import numpy as np
import ml_dtypes


def mxq(x, axis, fmt="e4m3"):
    dtype, down = {"e4m3": (ml_dtypes.float8_e4m3fn, 7), "e5m2": (ml_dtypes.float8_e5m2, 14)}[fmt]
    v = np.moveaxis(np.asarray(x, np.float32).astype(ml_dtypes.bfloat16).astype(np.float64), axis, -1)
    blocks = v.reshape(v.shape[:-1] + (-1, 32))
    amax = np.abs(blocks).max(-1, keepdims=True)
    byte = np.maximum(np.where(amax > 0, np.frexp(amax)[1] - 1 + 127, 0) - down, 1)
    scale = np.exp2(byte - 127.0)
    codes = (blocks / scale).astype(np.float32).astype(dtype).astype(np.float64)
    return np.moveaxis((codes * scale).reshape(v.shape), -1, axis)


WIDE = False


def mx_kscale(k):
    if not WIDE:
        return np.ones(k)
    levels = np.array([10, -10, 5, -5, 0])
    a = np.random.permutation(np.resize(levels, k // 512 * 4)).reshape(k // 512, 4)
    idx = np.arange(k)
    return np.exp2(a[idx // 512, idx % 128 // 32])


BF16 = ml_dtypes.bfloat16


def bf(x):
    return np.asarray(x, np.float32).astype(BF16)


def f64(x):
    return np.asarray(x).astype(np.float64)


B, F, D, L1, L2, L3 = 32, 64, 32, 256, 256, 256
H2 = L2 // 2
K3 = H2 * F


def interact(h, x0):
    z = h.transpose(0, 2, 1)[:, :, :, None] * x0.transpose(0, 2, 1)[:, :, None, :]
    return z.reshape(z.shape[0], z.shape[1], -1)


def setup_inputs():
    a = mx_kscale(K3).reshape(H2, F)[:, 0]
    return {"h2": bf(np.maximum(np.random.standard_normal((B, H2, D)) * 0.75, 0.0) * a[None, :, None]),
            "x0": bf(np.random.standard_normal((B, F, D))),
            "W3": bf(np.random.standard_normal((K3, L3)) / np.sqrt(K3) / np.repeat(a, F)[:, None]),
            "b3": bf(np.random.standard_normal(L3) * 0.2)}


def reference(h2, x0, W3, b3):
    z = interact(f64(h2), f64(x0))
    y = np.maximum((mxq(z, 2, "e4m3") @ mxq(f64(W3), 0, "e4m3")) + f64(b3), 0.0)
    return y.transpose(0, 2, 1).sum(axis=2)

@@ -1,0 +1,207 @@
+from contextlib import ExitStack
+
+import concourse.mybir as mybir
+from concourse.masks import make_identity
+
+FP8X4 = mybir.dt.float8_e4m3fn_x4
+BF16 = mybir.dt.bfloat16
+F32 = mybir.dt.float32
+U32 = mybir.dt.uint32
+U8 = mybir.dt.uint8
+MULT = mybir.AluOpType.mult
+ADD = mybir.AluOpType.add
+
+P = 128
+NB = 32
+ND = 32
+NW = NB * ND
+NC = 256
+NI = 8
+NT = 2
+HALF = 512
+
+FLOPS = 2 * NW * 8192 * NC
+
+
+def tile_cin_pb_kernel(tc, h2, x0, W3, b3, out):
+    nc = tc.nc
+    with ExitStack() as ctx:
+        const = ctx.enter_context(tc.tile_pool(name="const", bufs=1))
+        wgp = ctx.enter_context(tc.tile_pool(name="wgp", bufs=2))
+        h2p = ctx.enter_context(tc.tile_pool(name="h2p", bufs=4))
+        zbp = ctx.enter_context(tc.tile_pool(name="zbp", bufs=3))
+        zcp = ctx.enter_context(tc.tile_pool(name="zcp", bufs=10))
+        epi = ctx.enter_context(tc.tile_pool(name="epi", bufs=2))
+        accp = ctx.enter_context(tc.psum_pool(name="accp", bufs=1))
+        hpsp = ctx.enter_context(tc.psum_pool(name="hpsp", bufs=2))
+        miscp = ctx.enter_context(tc.psum_pool(name="miscp", bufs=1))
+
+        h2t = const.tile([P, NB, ND], BF16, name="h2t")
+        xraw = const.tile([P, NB, 256], BF16, name="xraw")
+        wraw = const.tile([P, NI, 2048], BF16, name="wraw")
+        bz = const.tile([P, P], BF16, name="bz")
+        h2v = h2.rearrange("b f d -> f b d")
+        xv = x0.rearrange("b (ga r) d -> ga b (r d)", ga=8)
+        wv = W3.rearrange("(i p r) c -> p i (r c)", i=NI, p=P, r=8)
+
+        nc.gpsimd.memset(bz[:], 0.0)
+        nc.scalar.dma_start(out=bz[0:2, :], in_=b3.rearrange("(ct c) -> ct c", ct=2))
+        for h in range(2):
+            bs = slice(16 * h, 16 * h + 16)
+            nc.sync.dma_start(out=h2t[:, bs, :], in_=h2v[:, bs, :])
+            for ga in range(8):
+                nc.sync.dma_start(
+                    out=xraw[ga:P:8, bs, :],
+                    in_=xv[ga : ga + 1, bs, :].to_broadcast([16, 16, 256]),
+                )
+        for i in range(NI):
+            nc.sync.dma_start(out=wraw[:, i, :], in_=wv[:, i, :])
+
+        ident_bf = const.tile([P, P], BF16, name="ident_bf")
+        make_identity(nc, ident_bf[:])
+        ident_f = const.tile([P, P], F32, name="ident_f")
+        make_identity(nc, ident_f[:])
+        sel = const.tile([P, NI, P], BF16, name="sel")
+        nc.vector.tensor_copy(
+            out=sel[:].rearrange("p i (ph r) -> p i ph r", r=8),
+            in_=ident_bf[:]
+            .rearrange("p (i ph) -> p i ph", i=NI)
+            .unsqueeze(3)
+            .to_broadcast([P, NI, 16, 8]),
+        )
+        res = const.tile([P, 2, P], F32, name="res")
+        nc.gpsimd.memset(res[:], 0.0)
+        bps = miscp.tile([P, P], BF16, name="bps", tag="misc")
+        nc.tensor.transpose(out=bps[:], in_=bz[:], identity=ident_bf[:])
+        b3f = const.tile([P, 2], F32, name="b3f")
+        nc.vector.tensor_copy(out=b3f[:], in_=bps[:, 0:2])
+
+        xg = const.tile([P, NT, NW, 4], BF16, name="xg")
+        wc = const.tile([P, NI * NT, NC], U32, name="wc", align_bytes=64)
+        ws = const.tile([P, NI * NT, NC], U8, name="ws", align_bytes=64)
+        acc = [
+            [accp.tile([P, HALF], F32, name="acc%d%d" % (ct, h)) for h in range(2)]
+            for ct in range(2)
+        ]
+
+        units = [(i, t, 0) for i in range(2) for t in range(NT)]
+        units += [(i, t, 1) for i in range(2) for t in range(NT)]
+        units += [(i, t, h) for i in range(2, NI) for h in range(2) for t in range(NT)]
+        n_units = len(units)
+        first_of = {}
+        last_of = {}
+        for n, (i, t, h) in enumerate(units):
+            if h not in first_of:
+                first_of[h] = n
+            last_of[h] = n
+
+        have_x = set()
+        have_h = {}
+        have_w = set()
+        zb_of = {}
+
+        def prepare(n):
+            i, t, h = units[n]
+            if (t, h) not in have_x:
+                have_x.add((t, h))
+                eng_copy = nc.vector.tensor_copy if t == 0 else nc.scalar.copy
+                eng_copy(
+                    out=xg[:, t, h * HALF : (h + 1) * HALF, :].rearrange(
+                        "p (b d) j -> p b d j", d=ND
+                    ),
+                    in_=xraw[:, 16 * h : 16 * h + 16, t * 128 : (t + 1) * 128].rearrange(
+                        "p b (j d) -> p b d j", j=4
+                    ),
+                )
+            if (i, h) not in have_h:
+                hps = hpsp.tile([P, HALF], BF16, name="hps")
+                nc.tensor.matmul(
+                    out=hps[:],
+                    lhsT=sel[:, i, :],
+                    rhs=h2t[:, 16 * h : 16 * h + 16, :].rearrange("p b d -> p (b d)"),
+                    start=True,
+                    stop=True,
+                )
+                hd = h2p.tile([P, HALF, 2], BF16, name="hd")
+                nc.scalar.copy(
+                    out=hd[:], in_=hps[:].unsqueeze(2).to_broadcast([P, HALF, 2])
+                )
+                have_h[(i, h)] = hd
+            zb = zbp.tile([P, HALF * 4], BF16, name="zb", align_bytes=64)
+            nc.vector.tensor_tensor(
+                out=zb[:].rearrange("p (w a e) -> p w a e", a=2, e=2),
+                in0=xg[:, t, h * HALF : (h + 1) * HALF, :].rearrange(
+                    "p w (a e) -> p w a e", a=2
+                ),
+                in1=have_h[(i, h)][:].unsqueeze(2).to_broadcast([P, HALF, 2, 2]),
+                op=MULT,
+            )
+            zb_of[n] = zb
+
+        def weights(i):
+            wg = wgp.tile([P, NT, NC, 4], BF16, name="wg", align_bytes=64)
+            for t in range(NT):
+                nc.scalar.copy(
+                    out=wg[:, t, :, :].rearrange("p (c q) j -> p c j q", q=4),
+                    in_=wraw[:, i, t * 1024 : (t + 1) * 1024].rearrange(
+                        "p (j c q) -> p c j q", j=4, q=4
+                    ),
+                )
+            nc.vector.quantize_mx(
+                out=wc[:, NT * i : NT * i + NT, :]
+                .rearrange("p s c -> p (s c)")
+                .bitcast(FP8X4),
+                scales=ws[:, NT * i : NT * i + NT, :].rearrange("p s c -> p (s c)"),
+                in_=wg[:].rearrange("p t c j -> p (t c j)"),
+            )
+
+        def finish(n):
+            i, t, h = units[n]
+            zc = zcp.tile([P, HALF], U32, name="zc", align_bytes=64)
+            zs = zcp.tile([P, HALF], U8, name="zs", align_bytes=64)
+            nc.vector.quantize_mx(out=zc[:].bitcast(FP8X4), scales=zs[:], in_=zb_of[n][:])
+            if i not in have_w:
+                have_w.add(i)
+                weights(i)
+            s = NT * i + t
+            for ct in range(2):
+                nc.tensor.matmul_mx(
+                    out=acc[ct][h][:],
+                    lhsT=wc[:, s, ct * P : (ct + 1) * P].bitcast(FP8X4),
+                    lhsT_scale=ws[:, s, ct * P : (ct + 1) * P],
+                    rhs=zc[:].bitcast(FP8X4),
+                    rhs_scale=zs[:],
+                    start=(n == first_of[h]),
+                    stop=(n == last_of[h]),
+                )
+            if n == last_of[h]:
+                for ct in range(2):
+                    y = epi.tile([P, 16, ND], F32, name="y")
+                    nc.scalar.activation(
+                        out=y[:].rearrange("p b d -> p (b d)"),
+                        in_=acc[ct][h][:],
+                        func=mybir.ActivationFunctionType.Relu,
+                        bias=b3f[:, ct : ct + 1],
+                        scale=1.0,
+                    )
+                    nc.vector.tensor_reduce(
+                        out=res[:, ct, 16 * h : 16 * h + 16],
+                        in_=y[:],
+                        axis=mybir.AxisListType.X,
+                        op=ADD,
+                    )
+
+        for n in range(n_units + 1):
+            if n < n_units:
+                prepare(n)
+            if n > 0:
+                finish(n - 1)
+
+        tps = miscp.tile([P, 2 * P], F32, name="tps", tag="misc")
+        for ct in range(2):
+            nc.tensor.transpose(
+                out=tps[:, ct * P : (ct + 1) * P], in_=res[:, ct, :], identity=ident_f[:]
+            )
+        o_sb = const.tile([NB, NC], F32, name="o_sb")
+        nc.scalar.copy(out=o_sb[:], in_=tps[0:NB, :])
+        nc.sync.dma_start(out=out[:, :], in_=o_sb[:])

@@ -10,6 +10,7 @@ U32 = mybir.dt.uint32
 U8 = mybir.dt.uint8
 MULT = mybir.AluOpType.mult
 ADD = mybir.AluOpType.add
+RELU = mybir.ActivationFunctionType.Relu
 
 P = 128
 NB = 32
@@ -19,6 +20,9 @@ NC = 256
 NI = 8
 NT = 2
 HALF = 512
+QUART = 256
+N_UNITS = 2 * NI * NT
+H_AHEAD = 3
 
 FLOPS = 2 * NW * 8192 * NC
 
@@ -26,119 +30,70 @@ FLOPS = 2 * NW * 8192 * NC
 def tile_cin_pb_kernel(tc, h2, x0, W3, b3, out):
     nc = tc.nc
     with ExitStack() as ctx:
+        ctx.enter_context(tc.manual_schedule())
         const = ctx.enter_context(tc.tile_pool(name="const", bufs=1))
-        wgp = ctx.enter_context(tc.tile_pool(name="wgp", bufs=2))
-        h2p = ctx.enter_context(tc.tile_pool(name="h2p", bufs=4))
+        wgp = ctx.enter_context(tc.tile_pool(name="wgp", bufs=NI))
         zbp = ctx.enter_context(tc.tile_pool(name="zbp", bufs=3))
-        zcp = ctx.enter_context(tc.tile_pool(name="zcp", bufs=10))
+        zcp = ctx.enter_context(tc.tile_pool(name="zcp", bufs=12))
         epi = ctx.enter_context(tc.tile_pool(name="epi", bufs=2))
         accp = ctx.enter_context(tc.psum_pool(name="accp", bufs=1))
-        hpsp = ctx.enter_context(tc.psum_pool(name="hpsp", bufs=2))
+        hpsp = ctx.enter_context(tc.psum_pool(name="hpsp", bufs=H_AHEAD))
         miscp = ctx.enter_context(tc.psum_pool(name="miscp", bufs=1))
 
-        h2t = const.tile([P, NB, ND], BF16, name="h2t")
+        h2t = const.tile([P, NW], BF16, name="h2t")
+        h2d = const.tile([P, NW, 2], BF16, name="h2d")
         xraw = const.tile([P, NB, 256], BF16, name="xraw")
         wraw = const.tile([P, NI, 2048], BF16, name="wraw")
         bz = const.tile([P, P], BF16, name="bz")
-        h2v = h2.rearrange("b f d -> f b d")
-        xv = x0.rearrange("b (ga r) d -> ga b (r d)", ga=8)
-        wv = W3.rearrange("(i p r) c -> p i (r c)", i=NI, p=P, r=8)
-
-        nc.gpsimd.memset(bz[:], 0.0)
-        nc.scalar.dma_start(out=bz[0:2, :], in_=b3.rearrange("(ct c) -> ct c", ct=2))
-        for h in range(2):
-            bs = slice(16 * h, 16 * h + 16)
-            nc.sync.dma_start(out=h2t[:, bs, :], in_=h2v[:, bs, :])
-            for ga in range(8):
-                nc.sync.dma_start(
-                    out=xraw[ga:P:8, bs, :],
-                    in_=xv[ga : ga + 1, bs, :].to_broadcast([16, 16, 256]),
-                )
-        for i in range(NI):
-            nc.sync.dma_start(out=wraw[:, i, :], in_=wv[:, i, :])
-
-        ident_bf = const.tile([P, P], BF16, name="ident_bf")
-        make_identity(nc, ident_bf[:])
-        ident_f = const.tile([P, P], F32, name="ident_f")
-        make_identity(nc, ident_f[:])
-        sel = const.tile([P, NI, P], BF16, name="sel")
-        nc.vector.tensor_copy(
-            out=sel[:].rearrange("p i (ph r) -> p i ph r", r=8),
-            in_=ident_bf[:]
-            .rearrange("p (i ph) -> p i ph", i=NI)
-            .unsqueeze(3)
-            .to_broadcast([P, NI, 16, 8]),
-        )
-        res = const.tile([P, 2, P], F32, name="res")
-        nc.gpsimd.memset(res[:], 0.0)
-        bps = miscp.tile([P, P], BF16, name="bps", tag="misc")
-        nc.tensor.transpose(out=bps[:], in_=bz[:], identity=ident_bf[:])
-        b3f = const.tile([P, 2], F32, name="b3f")
-        nc.vector.tensor_copy(out=b3f[:], in_=bps[:, 0:2])
-
         xg = const.tile([P, NT, NW, 4], BF16, name="xg")
         wc = const.tile([P, NI * NT, NC], U32, name="wc", align_bytes=64)
         ws = const.tile([P, NI * NT, NC], U8, name="ws", align_bytes=64)
+        ident_bf = const.tile([P, P], BF16, name="ident_bf")
+        ident_f = const.tile([P, P], F32, name="ident_f")
+        sel = const.tile([P, NI, P], F32, name="sel")
+        res = const.tile([P, 2, P], F32, name="res")
+        b3f = const.tile([P, 2], F32, name="b3f")
+        junk = const.tile([P, ND], F32, name="junk")
+        o_sb = const.tile([NB, NC], F32, name="o_sb")
         acc = [
             [accp.tile([P, HALF], F32, name="acc%d%d" % (ct, h)) for h in range(2)]
             for ct in range(2)
         ]
 
-        units = [(i, t, 0) for i in range(2) for t in range(NT)]
-        units += [(i, t, 1) for i in range(2) for t in range(NT)]
-        units += [(i, t, h) for i in range(2, NI) for h in range(2) for t in range(NT)]
-        n_units = len(units)
-        first_of = {}
-        last_of = {}
-        for n, (i, t, h) in enumerate(units):
-            if h not in first_of:
-                first_of[h] = n
-            last_of[h] = n
+        h2v = h2.rearrange("b f d -> f b d")
+        xv = x0.rearrange("b (ga r) d -> ga b (r d)", ga=8)
+        wv = W3.rearrange("(i p r) c -> p i (r c)", i=NI, p=P, r=8)
 
-        have_x = set()
-        have_h = {}
-        have_w = set()
-        zb_of = {}
-
-        def prepare(n):
-            i, t, h = units[n]
-            if (t, h) not in have_x:
-                have_x.add((t, h))
-                eng_copy = nc.vector.tensor_copy if t == 0 else nc.scalar.copy
-                eng_copy(
-                    out=xg[:, t, h * HALF : (h + 1) * HALF, :].rearrange(
-                        "p (b d) j -> p b d j", d=ND
-                    ),
-                    in_=xraw[:, 16 * h : 16 * h + 16, t * 128 : (t + 1) * 128].rearrange(
-                        "p b (j d) -> p b d j", j=4
-                    ),
-                )
-            if (i, h) not in have_h:
-                hps = hpsp.tile([P, HALF], BF16, name="hps")
-                nc.tensor.matmul(
-                    out=hps[:],
-                    lhsT=sel[:, i, :],
-                    rhs=h2t[:, 16 * h : 16 * h + 16, :].rearrange("p b d -> p (b d)"),
-                    start=True,
-                    stop=True,
-                )
-                hd = h2p.tile([P, HALF, 2], BF16, name="hd")
-                nc.scalar.copy(
-                    out=hd[:], in_=hps[:].unsqueeze(2).to_broadcast([P, HALF, 2])
-                )
-                have_h[(i, h)] = hd
-            zb = zbp.tile([P, HALF * 4], BF16, name="zb", align_bytes=64)
-            nc.vector.tensor_tensor(
-                out=zb[:].rearrange("p (w a e) -> p w a e", a=2, e=2),
-                in0=xg[:, t, h * HALF : (h + 1) * HALF, :].rearrange(
-                    "p w (a e) -> p w a e", a=2
-                ),
-                in1=have_h[(i, h)][:].unsqueeze(2).to_broadcast([P, HALF, 2, 2]),
-                op=MULT,
+        def load_h(h):
+            return dict(
+                out=h2t[:, h * HALF : (h + 1) * HALF].rearrange("p (b d) -> p b d", d=ND),
+                in_=h2v[:, 16 * h : 16 * h + 16, :],
             )
-            zb_of[n] = zb
 
-        def weights(i):
+        def load_x(b0, nb):
+            for ga in range(8):
+                nc.sync.dma_start(
+                    out=xraw[ga:P:8, b0 : b0 + nb, :],
+                    in_=xv[ga : ga + 1, b0 : b0 + nb, :].to_broadcast([16, nb, 256]),
+                )
+
+        def dup_h(copy, h):
+            copy(
+                out=h2d[:, h * HALF : (h + 1) * HALF, :],
+                in_=h2t[:, h * HALF : (h + 1) * HALF].unsqueeze(2).to_broadcast([P, HALF, 2]),
+            )
+
+        def regroup_x(copy, t, b0, nb):
+            copy(
+                out=xg[:, t, b0 * ND : (b0 + nb) * ND, :].rearrange("p (b d) j -> p b d j", d=ND),
+                in_=xraw[:, b0 : b0 + nb, t * 128 : (t + 1) * 128].rearrange(
+                    "p b (j d) -> p b d j", j=4
+                ),
+            )
+
+        wg_of = {}
+
+        def regroup_w(i):
             wg = wgp.tile([P, NT, NC, 4], BF16, name="wg", align_bytes=64)
             for t in range(NT):
                 nc.scalar.copy(
@@ -147,23 +102,67 @@ def tile_cin_pb_kernel(tc, h2, x0, W3, b3, out):
                         "p (j c q) -> p c j q", j=4, q=4
                     ),
                 )
+            wg_of[i] = wg
+
+        def quantise_w(i):
             nc.vector.quantize_mx(
-                out=wc[:, NT * i : NT * i + NT, :]
-                .rearrange("p s c -> p (s c)")
-                .bitcast(FP8X4),
+                out=wc[:, NT * i : NT * i + NT, :].rearrange("p s c -> p (s c)").bitcast(FP8X4),
                 scales=ws[:, NT * i : NT * i + NT, :].rearrange("p s c -> p (s c)"),
-                in_=wg[:].rearrange("p t c j -> p (t c j)"),
+                in_=wg_of[i][:].rearrange("p t c j -> p (t c j)"),
             )
 
-        def finish(n):
-            i, t, h = units[n]
+        hps_of = {}
+
+        def spread_h(r, pieces):
+            h, i = divmod(r, NI)
+            hps = hpsp.tile([P, HALF], F32, name="hps")
+            step = HALF // pieces
+            for k in range(pieces):
+                nc.tensor.matmul(
+                    out=hps[:, k * step : (k + 1) * step],
+                    lhsT=sel[:, i, :],
+                    rhs=h2d[:, h * HALF + k * step : h * HALF + (k + 1) * step, :]
+                    .rearrange("p w e -> p (w e)")
+                    .bitcast(F32),
+                    start=True,
+                    stop=True,
+                )
+            hps_of[r] = hps
+
+        zb_of = {}
+        zq_of = {}
+
+        def multiply(n, w0, nw):
+            r, t = divmod(n, NT)
+            h = r // NI
+            if n not in zb_of:
+                zb_of[n] = zbp.tile([P, HALF * 4], BF16, name="zb", align_bytes=64)
+            nc.vector.tensor_tensor(
+                out=zb_of[n][:, w0 * 4 : (w0 + nw) * 4].rearrange(
+                    "p (w a e) -> p w a e", a=2, e=2
+                ),
+                in0=xg[:, t, h * HALF + w0 : h * HALF + w0 + nw, :].rearrange(
+                    "p w (a e) -> p w a e", a=2
+                ),
+                in1=hps_of[r][:, w0 : w0 + nw]
+                .bitcast(BF16)
+                .rearrange("p (w e) -> p w e", e=2)
+                .unsqueeze(2)
+                .to_broadcast([P, nw, 2, 2]),
+                op=MULT,
+            )
+
+        def quantise_z(n):
             zc = zcp.tile([P, HALF], U32, name="zc", align_bytes=64)
             zs = zcp.tile([P, HALF], U8, name="zs", align_bytes=64)
             nc.vector.quantize_mx(out=zc[:].bitcast(FP8X4), scales=zs[:], in_=zb_of[n][:])
-            if i not in have_w:
-                have_w.add(i)
-                weights(i)
+            zq_of[n] = (zc, zs)
+
+        def contract(n):
+            r, t = divmod(n, NT)
+            h, i = divmod(r, NI)
             s = NT * i + t
+            zc, zs = zq_of[n]
             for ct in range(2):
                 nc.tensor.matmul_mx(
                     out=acc[ct][h][:],
@@ -171,37 +170,97 @@ def tile_cin_pb_kernel(tc, h2, x0, W3, b3, out):
                     lhsT_scale=ws[:, s, ct * P : (ct + 1) * P],
                     rhs=zc[:].bitcast(FP8X4),
                     rhs_scale=zs[:],
-                    start=(n == first_of[h]),
-                    stop=(n == last_of[h]),
+                    start=(s == 0),
+                    stop=(s == NI * NT - 1),
                 )
-            if n == last_of[h]:
-                for ct in range(2):
-                    y = epi.tile([P, 16, ND], F32, name="y")
-                    nc.scalar.activation(
-                        out=y[:].rearrange("p b d -> p (b d)"),
-                        in_=acc[ct][h][:],
-                        func=mybir.ActivationFunctionType.Relu,
-                        bias=b3f[:, ct : ct + 1],
-                        scale=1.0,
-                    )
-                    nc.vector.tensor_reduce(
-                        out=res[:, ct, 16 * h : 16 * h + 16],
-                        in_=y[:],
-                        axis=mybir.AxisListType.X,
-                        op=ADD,
-                    )
 
-        for n in range(n_units + 1):
-            if n < n_units:
-                prepare(n)
-            if n > 0:
-                finish(n - 1)
+        nc.gpsimd.memset(bz[:], 0.0)
+        nc.scalar.dma_start(**load_h(0))
+        nc.scalar.dma_start(out=bz[0:2, :], in_=b3.rearrange("(ct c) -> ct c", ct=2))
+        load_x(0, 8)
+        load_x(8, 8)
+        for i in range(NI):
+            nc.sync.dma_start(out=wraw[:, i, :], in_=wv[:, i, :])
+        nc.sync.dma_start(**load_h(1))
+        load_x(16, 16)
 
+        make_identity(nc, ident_f[:])
+        make_identity(nc, ident_bf[:])
+        nc.gpsimd.memset(res[:], 0.0)
+        nc.vector.tensor_copy(
+            out=sel[:].rearrange("p i (ph r) -> p i ph r", r=8),
+            in_=ident_f[:]
+            .rearrange("p (i ph) -> p i ph", i=NI)
+            .unsqueeze(3)
+            .to_broadcast([P, NI, 16, 8]),
+        )
+        dup_h(nc.vector.tensor_copy, 0)
+        spread_h(0, 2)
+        spread_h(1, 1)
+        spread_h(2, 1)
+        bps = miscp.tile([P, P], BF16, name="bps", tag="misc")
+        nc.tensor.transpose(out=bps[:], in_=bz[:], identity=ident_bf[:])
+
+        regroup_x(nc.scalar.copy, 1, 0, 8)
+        regroup_x(nc.scalar.copy, 1, 8, 8)
+        nc.scalar.copy(out=b3f[:], in_=bps[:, 0:2])
+        for i in range(6):
+            regroup_w(i)
+        dup_h(nc.scalar.copy, 1)
+        regroup_x(nc.scalar.copy, 0, 16, 16)
+        regroup_w(6)
+        regroup_x(nc.scalar.copy, 1, 16, 16)
+        regroup_w(7)
+
+        for k in range(2):
+            regroup_x(nc.vector.tensor_copy, 0, 8 * k, 8)
+            multiply(0, k * QUART, QUART)
+            multiply(1, k * QUART, QUART)
+        spread_h(H_AHEAD, 1)
+
+        contracted = 0
+        w_done = 0
+        for n in range(N_UNITS):
+            if 1 <= n < N_UNITS - 1:
+                multiply(n + 1, 0, HALF)
+                if (n + 1) % NT == NT - 1 and (n + 1) // NT + H_AHEAD < 2 * NI:
+                    spread_h((n + 1) // NT + H_AHEAD, 1)
+            quantise_z(n)
+            if n >= 3 and n % 2 == 1 and w_done < NI:
+                quantise_w(w_done)
+                w_done += 1
+            while contracted <= n and (contracted // NT) % NI < w_done:
+                m = contracted
+                contracted += 1
+                contract(m)
+                if m == NI * NT - 1:
+                    for ct in range(2):
+                        for b in range(16):
+                            nc.scalar.activation(
+                                out=junk[:],
+                                in_=acc[ct][0][:, b * ND : (b + 1) * ND],
+                                func=RELU,
+                                bias=b3f[:, ct : ct + 1],
+                                scale=1.0,
+                                accum_out=res[:, ct, b : b + 1],
+                            )
+
+        for ct in range(2):
+            y = epi.tile([P, 16, ND], F32, name="y")
+            nc.scalar.activation(
+                out=y[:].rearrange("p b d -> p (b d)"),
+                in_=acc[ct][1][:],
+                func=RELU,
+                bias=b3f[:, ct : ct + 1],
+                scale=1.0,
+            )
+            nc.vector.tensor_reduce(
+                out=res[:, ct, 16:32], in_=y[:], axis=mybir.AxisListType.X, op=ADD
+            )
         tps = miscp.tile([P, 2 * P], F32, name="tps", tag="misc")
         for ct in range(2):
             nc.tensor.transpose(
                 out=tps[:, ct * P : (ct + 1) * P], in_=res[:, ct, :], identity=ident_f[:]
             )
-        o_sb = const.tile([NB, NC], F32, name="o_sb")
         nc.scalar.copy(out=o_sb[:], in_=tps[0:NB, :])
         nc.sync.dma_start(out=out[:, :], in_=o_sb[:])

@@ -21,7 +21,7 @@ NI = 8
 NT = 2
 HALF = 512
 QUART = 256
-N_UNITS = 2 * NI * NT
+N_PAIRS = 2 * NI
 H_AHEAD = 3
 
 FLOPS = 2 * NW * 8192 * NC
@@ -32,9 +32,9 @@ def tile_cin_pb_kernel(tc, h2, x0, W3, b3, out):
     with ExitStack() as ctx:
         ctx.enter_context(tc.manual_schedule())
         const = ctx.enter_context(tc.tile_pool(name="const", bufs=1))
-        wgp = ctx.enter_context(tc.tile_pool(name="wgp", bufs=NI))
-        zbp = ctx.enter_context(tc.tile_pool(name="zbp", bufs=3))
-        zcp = ctx.enter_context(tc.tile_pool(name="zcp", bufs=12))
+        wgp = ctx.enter_context(tc.tile_pool(name="wgp", bufs=NI // 2))
+        zbp = ctx.enter_context(tc.tile_pool(name="zbp", bufs=4))
+        zcp = ctx.enter_context(tc.tile_pool(name="zcp", bufs=6))
         epi = ctx.enter_context(tc.tile_pool(name="epi", bufs=2))
         accp = ctx.enter_context(tc.psum_pool(name="accp", bufs=1))
         hpsp = ctx.enter_context(tc.psum_pool(name="hpsp", bufs=H_AHEAD))
@@ -51,6 +51,7 @@ def tile_cin_pb_kernel(tc, h2, x0, W3, b3, out):
         ident_bf = const.tile([P, P], BF16, name="ident_bf")
         ident_f = const.tile([P, P], F32, name="ident_f")
         sel = const.tile([P, NI, P], F32, name="sel")
+        sel_bf = const.tile([P, H_AHEAD, P], BF16, name="sel_bf")
         res = const.tile([P, 2, P], F32, name="res")
         b3f = const.tile([P, 2], F32, name="b3f")
         junk = const.tile([P, ND], F32, name="junk")
@@ -70,17 +71,19 @@ def tile_cin_pb_kernel(tc, h2, x0, W3, b3, out):
                 in_=h2v[:, 16 * h : 16 * h + 16, :],
             )
 
-        def load_x(b0, nb):
+        def load_x(queues, b0, nb, c0, ncol):
             for ga in range(8):
-                nc.sync.dma_start(
-                    out=xraw[ga:P:8, b0 : b0 + nb, :],
-                    in_=xv[ga : ga + 1, b0 : b0 + nb, :].to_broadcast([16, nb, 256]),
+                queues[ga % len(queues)].dma_start(
+                    out=xraw[ga:P:8, b0 : b0 + nb, c0 : c0 + ncol],
+                    in_=xv[ga : ga + 1, b0 : b0 + nb, c0 : c0 + ncol].to_broadcast(
+                        [16, nb, ncol]
+                    ),
                 )
 
-        def dup_h(copy, h):
+        def dup_h(copy, w0, nw):
             copy(
-                out=h2d[:, h * HALF : (h + 1) * HALF, :],
-                in_=h2t[:, h * HALF : (h + 1) * HALF].unsqueeze(2).to_broadcast([P, HALF, 2]),
+                out=h2d[:, w0 : w0 + nw, :],
+                in_=h2t[:, w0 : w0 + nw].unsqueeze(2).to_broadcast([P, nw, 2]),
             )
 
         def regroup_x(copy, t, b0, nb):
@@ -94,34 +97,43 @@ def tile_cin_pb_kernel(tc, h2, x0, W3, b3, out):
         wg_of = {}
 
         def regroup_w(i):
-            wg = wgp.tile([P, NT, NC, 4], BF16, name="wg", align_bytes=64)
+            if i // 2 not in wg_of:
+                wg_of[i // 2] = wgp.tile([P, 2 * NT, NC, 4], BF16, name="wg", align_bytes=64)
+            wg = wg_of[i // 2]
             for t in range(NT):
                 nc.scalar.copy(
-                    out=wg[:, t, :, :].rearrange("p (c q) j -> p c j q", q=4),
+                    out=wg[:, NT * (i % 2) + t, :, :].rearrange("p (c q) j -> p c j q", q=4),
                     in_=wraw[:, i, t * 1024 : (t + 1) * 1024].rearrange(
                         "p (j c q) -> p c j q", j=4, q=4
                     ),
                 )
-            wg_of[i] = wg
 
-        def quantise_w(i):
+        def quantise_w(ii):
             nc.vector.quantize_mx(
-                out=wc[:, NT * i : NT * i + NT, :].rearrange("p s c -> p (s c)").bitcast(FP8X4),
-                scales=ws[:, NT * i : NT * i + NT, :].rearrange("p s c -> p (s c)"),
-                in_=wg_of[i][:].rearrange("p t c j -> p (t c j)"),
+                out=wc[:, 4 * ii : 4 * ii + 4, :].rearrange("p s c -> p (s c)").bitcast(FP8X4),
+                scales=ws[:, 4 * ii : 4 * ii + 4, :].rearrange("p s c -> p (s c)"),
+                in_=wg_of[ii][:].rearrange("p s c j -> p (s c j)"),
             )
 
         hps_of = {}
 
-        def spread_h(r, pieces):
+        def spread_h(r):
             h, i = divmod(r, NI)
             hps = hpsp.tile([P, HALF], F32, name="hps")
-            step = HALF // pieces
-            for k in range(pieces):
+            if r < H_AHEAD:
+                for k in range(2):
+                    nc.tensor.matmul(
+                        out=hps[:, k * QUART : (k + 1) * QUART].bitcast(BF16),
+                        lhsT=sel_bf[:, i, :],
+                        rhs=h2d[:, k * QUART : (k + 1) * QUART, :].rearrange("p w e -> p (w e)"),
+                        start=True,
+                        stop=True,
+                    )
+            else:
                 nc.tensor.matmul(
-                    out=hps[:, k * step : (k + 1) * step],
+                    out=hps[:],
                     lhsT=sel[:, i, :],
-                    rhs=h2d[:, h * HALF + k * step : h * HALF + (k + 1) * step, :]
+                    rhs=h2d[:, h * HALF : (h + 1) * HALF, :]
                     .rearrange("p w e -> p (w e)")
                     .bitcast(F32),
                     start=True,
@@ -132,13 +144,12 @@ def tile_cin_pb_kernel(tc, h2, x0, W3, b3, out):
         zb_of = {}
         zq_of = {}
 
-        def multiply(n, w0, nw):
-            r, t = divmod(n, NT)
+        def multiply(r, t, w0, nw):
             h = r // NI
-            if n not in zb_of:
-                zb_of[n] = zbp.tile([P, HALF * 4], BF16, name="zb", align_bytes=64)
+            if r not in zb_of:
+                zb_of[r] = zbp.tile([P, NT, HALF * 4], BF16, name="zb", align_bytes=64)
             nc.vector.tensor_tensor(
-                out=zb_of[n][:, w0 * 4 : (w0 + nw) * 4].rearrange(
+                out=zb_of[r][:, t, w0 * 4 : (w0 + nw) * 4].rearrange(
                     "p (w a e) -> p w a e", a=2, e=2
                 ),
                 in0=xg[:, t, h * HALF + w0 : h * HALF + w0 + nw, :].rearrange(
@@ -152,41 +163,65 @@ def tile_cin_pb_kernel(tc, h2, x0, W3, b3, out):
                 op=MULT,
             )
 
-        def quantise_z(n):
-            zc = zcp.tile([P, HALF], U32, name="zc", align_bytes=64)
-            zs = zcp.tile([P, HALF], U8, name="zs", align_bytes=64)
-            nc.vector.quantize_mx(out=zc[:].bitcast(FP8X4), scales=zs[:], in_=zb_of[n][:])
-            zq_of[n] = (zc, zs)
+        def quantise_z(r, t0, nt):
+            if r not in zq_of:
+                zc = zcp.tile([P, NT * HALF], U32, name="zc", align_bytes=64)
+                zs = zcp.tile([P, NT * HALF], U8, name="zs", align_bytes=64)
+                zq_of[r] = (zc, zs)
+            zc, zs = zq_of[r]
+            nc.vector.quantize_mx(
+                out=zc[:, t0 * HALF : (t0 + nt) * HALF].bitcast(FP8X4),
+                scales=zs[:, t0 * HALF : (t0 + nt) * HALF],
+                in_=zb_of[r][:, t0 : t0 + nt, :].rearrange("p t w -> p (t w)"),
+            )
 
-        def contract(n):
-            r, t = divmod(n, NT)
+        def contract(r, t):
             h, i = divmod(r, NI)
             s = NT * i + t
-            zc, zs = zq_of[n]
+            zc, zs = zq_of[r]
             for ct in range(2):
                 nc.tensor.matmul_mx(
                     out=acc[ct][h][:],
                     lhsT=wc[:, s, ct * P : (ct + 1) * P].bitcast(FP8X4),
                     lhsT_scale=ws[:, s, ct * P : (ct + 1) * P],
-                    rhs=zc[:].bitcast(FP8X4),
-                    rhs_scale=zs[:],
+                    rhs=zc[:, t * HALF : (t + 1) * HALF].bitcast(FP8X4),
+                    rhs_scale=zs[:, t * HALF : (t + 1) * HALF],
                     start=(s == 0),
                     stop=(s == NI * NT - 1),
                 )
 
-        nc.gpsimd.memset(bz[:], 0.0)
+        def pool_first_half():
+            for ct in range(2):
+                for b in range(16):
+                    nc.scalar.activation(
+                        out=junk[:],
+                        in_=acc[ct][0][:, b * ND : (b + 1) * ND],
+                        func=RELU,
+                        bias=b3f[:, ct : ct + 1],
+                        scale=1.0,
+                        accum_out=res[:, ct, b : b + 1],
+                    )
+
         nc.scalar.dma_start(**load_h(0))
-        nc.scalar.dma_start(out=bz[0:2, :], in_=b3.rearrange("(ct c) -> ct c", ct=2))
-        load_x(0, 8)
-        load_x(8, 8)
+        load_x([nc.sync, nc.scalar], 0, 16, 0, 128)
+        load_x([nc.sync], 0, 16, 128, 128)
+        nc.sync.dma_start(**load_h(1))
         for i in range(NI):
             nc.sync.dma_start(out=wraw[:, i, :], in_=wv[:, i, :])
-        nc.sync.dma_start(**load_h(1))
-        load_x(16, 16)
-
-        make_identity(nc, ident_f[:])
         make_identity(nc, ident_bf[:])
+        make_identity(nc, ident_f[:])
+        nc.gpsimd.memset(bz[:], 0.0)
         nc.gpsimd.memset(res[:], 0.0)
+        nc.sync.dma_start(out=bz[0:2, :], in_=b3.rearrange("(ct c) -> ct c", ct=2))
+        load_x([nc.sync], 16, 16, 0, 256)
+
+        nc.vector.tensor_copy(
+            out=sel_bf[:].rearrange("p i (ph r) -> p i ph r", r=8),
+            in_=ident_bf[:, 0 : 16 * H_AHEAD]
+            .rearrange("p (i ph) -> p i ph", i=H_AHEAD)
+            .unsqueeze(3)
+            .to_broadcast([P, H_AHEAD, 16, 8]),
+        )
         nc.vector.tensor_copy(
             out=sel[:].rearrange("p i (ph r) -> p i ph r", r=8),
             in_=ident_f[:]
@@ -194,56 +229,61 @@ def tile_cin_pb_kernel(tc, h2, x0, W3, b3, out):
             .unsqueeze(3)
             .to_broadcast([P, NI, 16, 8]),
         )
-        dup_h(nc.vector.tensor_copy, 0)
-        spread_h(0, 2)
-        spread_h(1, 1)
-        spread_h(2, 1)
-        bps = miscp.tile([P, P], BF16, name="bps", tag="misc")
-        nc.tensor.transpose(out=bps[:], in_=bz[:], identity=ident_bf[:])
+        dup_h(nc.vector.tensor_copy, 0, QUART)
+        dup_h(nc.vector.tensor_copy, QUART, QUART)
+        for r in range(H_AHEAD):
+            spread_h(r)
 
+        regroup_x(nc.scalar.copy, 0, 8, 8)
         regroup_x(nc.scalar.copy, 1, 0, 8)
         regroup_x(nc.scalar.copy, 1, 8, 8)
-        nc.scalar.copy(out=b3f[:], in_=bps[:, 0:2])
-        for i in range(6):
+        regroup_w(0)
+        regroup_w(1)
+        dup_h(nc.scalar.copy, HALF, HALF)
+        for i in range(2, 5):
             regroup_w(i)
-        dup_h(nc.scalar.copy, 1)
         regroup_x(nc.scalar.copy, 0, 16, 16)
-        regroup_w(6)
         regroup_x(nc.scalar.copy, 1, 16, 16)
-        regroup_w(7)
+        for i in range(5, NI):
+            regroup_w(i)
 
-        for k in range(2):
-            regroup_x(nc.vector.tensor_copy, 0, 8 * k, 8)
-            multiply(0, k * QUART, QUART)
-            multiply(1, k * QUART, QUART)
-        spread_h(H_AHEAD, 1)
+        regroup_x(nc.vector.tensor_copy, 0, 0, 8)
+        for t in range(NT):
+            for r in range(H_AHEAD):
+                if r == 0:
+                    multiply(r, t, 0, QUART)
+                    multiply(r, t, QUART, QUART)
+                else:
+                    multiply(r, t, 0, HALF)
+                if t == NT - 1:
+                    spread_h(r + H_AHEAD)
 
         contracted = 0
         w_done = 0
-        for n in range(N_UNITS):
-            if 1 <= n < N_UNITS - 1:
-                multiply(n + 1, 0, HALF)
-                if (n + 1) % NT == NT - 1 and (n + 1) // NT + H_AHEAD < 2 * NI:
-                    spread_h((n + 1) // NT + H_AHEAD, 1)
-            quantise_z(n)
-            if n >= 3 and n % 2 == 1 and w_done < NI:
-                quantise_w(w_done)
-                w_done += 1
-            while contracted <= n and (contracted // NT) % NI < w_done:
-                m = contracted
+        for r in range(N_PAIRS):
+            if r == N_PAIRS - 1:
+                quantise_z(r, 0, 1)
+                quantise_z(r, 1, 1)
+            else:
+                quantise_z(r, 0, NT)
+            if r >= 2 and r % 2 == 0 and w_done < NI:
+                quantise_w(w_done // 2)
+                w_done += 2
+            if r + H_AHEAD < N_PAIRS:
+                for t in range(NT):
+                    multiply(r + H_AHEAD, t, 0, HALF)
+                if r + 2 * H_AHEAD < N_PAIRS:
+                    spread_h(r + 2 * H_AHEAD)
+            if r == 5:
+                bps = miscp.tile([P, P], BF16, name="bps", tag="misc")
+                nc.tensor.transpose(out=bps[:], in_=bz[:], identity=ident_bf[:])
+                nc.scalar.copy(out=b3f[:], in_=bps[:, 0:2])
+            while contracted <= r and contracted % NI < w_done:
+                for t in range(NT):
+                    contract(contracted, t)
                 contracted += 1
-                contract(m)
-                if m == NI * NT - 1:
-                    for ct in range(2):
-                        for b in range(16):
-                            nc.scalar.activation(
-                                out=junk[:],
-                                in_=acc[ct][0][:, b * ND : (b + 1) * ND],
-                                func=RELU,
-                                bias=b3f[:, ct : ct + 1],
-                                scale=1.0,
-                                accum_out=res[:, ct, b : b + 1],
-                            )
+                if contracted == NI:
+                    pool_first_half()
 
         for ct in range(2):
             y = epi.tile([P, 16, ND], F32, name="y")

@@ -23,6 +23,7 @@ HALF = 512
 QUART = 256
 N_PAIRS = 2 * NI
 H_AHEAD = 3
+G_COLS = 128
 
 FLOPS = 2 * NW * 8192 * NC
 
@@ -36,6 +37,7 @@ def tile_cin_pb_kernel(tc, h2, x0, W3, b3, out):
         zbp = ctx.enter_context(tc.tile_pool(name="zbp", bufs=4))
         zcp = ctx.enter_context(tc.tile_pool(name="zcp", bufs=6))
         epi = ctx.enter_context(tc.tile_pool(name="epi", bufs=2))
+        hgp = ctx.enter_context(tc.tile_pool(name="hgp", bufs=H_AHEAD + 1))
         accp = ctx.enter_context(tc.psum_pool(name="accp", bufs=1))
         hpsp = ctx.enter_context(tc.psum_pool(name="hpsp", bufs=H_AHEAD))
         miscp = ctx.enter_context(tc.psum_pool(name="miscp", bufs=1))
@@ -116,6 +118,7 @@ def tile_cin_pb_kernel(tc, h2, x0, W3, b3, out):
             )
 
         hps_of = {}
+        hg_of = {}
 
         def spread_h(r):
             h, i = divmod(r, NI)
@@ -139,6 +142,18 @@ def tile_cin_pb_kernel(tc, h2, x0, W3, b3, out):
                     start=True,
                     stop=True,
                 )
+                hgps = miscp.tile([P, G_COLS], F32, name="hgps", tag="misc")
+                nc.tensor.matmul(
+                    out=hgps[:],
+                    lhsT=sel[:, i, :],
+                    rhs=h2d[:, (h + 1) * HALF - G_COLS : (h + 1) * HALF, :]
+                    .rearrange("p w e -> p (w e)")
+                    .bitcast(F32),
+                    start=True,
+                    stop=True,
+                )
+                hg_of[r] = hgp.tile([P, G_COLS], F32, name="hg")
+                nc.scalar.copy(out=hg_of[r][:], in_=hgps[:])
             hps_of[r] = hps
 
         zb_of = {}
@@ -148,14 +163,22 @@ def tile_cin_pb_kernel(tc, h2, x0, W3, b3, out):
             h = r // NI
             if r not in zb_of:
                 zb_of[r] = zbp.tile([P, NT, HALF * 4], BF16, name="zb", align_bytes=64)
-            nc.vector.tensor_tensor(
+            if w0 + nw <= HALF:
+                engine = nc.vector
+                pairs = hps_of[r][:, w0 : w0 + nw]
+            else:
+                engine = nc.gpsimd
+                w0 = HALF - G_COLS
+                nw = G_COLS
+                pairs = hg_of[r][:]
+            engine.tensor_tensor(
                 out=zb_of[r][:, t, w0 * 4 : (w0 + nw) * 4].rearrange(
                     "p (w a e) -> p w a e", a=2, e=2
                 ),
                 in0=xg[:, t, h * HALF + w0 : h * HALF + w0 + nw, :].rearrange(
                     "p w (a e) -> p w a e", a=2
                 ),
-                in1=hps_of[r][:, w0 : w0 + nw]
+                in1=pairs
                 .bitcast(BF16)
                 .rearrange("p (w e) -> p w e", e=2)
                 .unsqueeze(2)
@@ -240,12 +263,6 @@ def tile_cin_pb_kernel(tc, h2, x0, W3, b3, out):
         regroup_w(0)
         regroup_w(1)
         dup_h(nc.scalar.copy, HALF, HALF)
-        for i in range(2, 5):
-            regroup_w(i)
-        regroup_x(nc.scalar.copy, 0, 16, 16)
-        regroup_x(nc.scalar.copy, 1, 16, 16)
-        for i in range(5, NI):
-            regroup_w(i)
 
         regroup_x(nc.vector.tensor_copy, 0, 0, 8)
         for t in range(NT):
@@ -261,6 +278,14 @@ def tile_cin_pb_kernel(tc, h2, x0, W3, b3, out):
         contracted = 0
         w_done = 0
         for r in range(N_PAIRS):
+            if r < 3:
+                regroup_w(r + 2)
+            elif r < 5:
+                regroup_x(nc.scalar.copy, r - 3, 16, 16)
+            elif r < 8:
+                regroup_w(r)
+            if r + H_AHEAD < N_PAIRS:
+                multiply(r + H_AHEAD, 1, HALF, 1)
             if r == N_PAIRS - 1:
                 quantise_z(r, 0, 1)
                 quantise_z(r, 1, 1)
@@ -270,8 +295,8 @@ def tile_cin_pb_kernel(tc, h2, x0, W3, b3, out):
                 quantise_w(w_done // 2)
                 w_done += 2
             if r + H_AHEAD < N_PAIRS:
-                for t in range(NT):
-                    multiply(r + H_AHEAD, t, 0, HALF)
+                multiply(r + H_AHEAD, 0, 0, HALF)
+                multiply(r + H_AHEAD, 1, 0, HALF - G_COLS)
                 if r + 2 * H_AHEAD < N_PAIRS:
                     spread_h(r + 2 * H_AHEAD)
             if r == 5:

@@ -23,7 +23,6 @@ HALF = 512
 QUART = 256
 N_PAIRS = 2 * NI
 H_AHEAD = 3
-G_COLS = 128
 
 FLOPS = 2 * NW * 8192 * NC
 
@@ -36,8 +35,7 @@ def tile_cin_pb_kernel(tc, h2, x0, W3, b3, out):
         wgp = ctx.enter_context(tc.tile_pool(name="wgp", bufs=NI // 2))
         zbp = ctx.enter_context(tc.tile_pool(name="zbp", bufs=4))
         zcp = ctx.enter_context(tc.tile_pool(name="zcp", bufs=6))
-        epi = ctx.enter_context(tc.tile_pool(name="epi", bufs=2))
-        hgp = ctx.enter_context(tc.tile_pool(name="hgp", bufs=H_AHEAD + 1))
+        epi = ctx.enter_context(tc.tile_pool(name="epi", bufs=4))
         accp = ctx.enter_context(tc.psum_pool(name="accp", bufs=1))
         hpsp = ctx.enter_context(tc.psum_pool(name="hpsp", bufs=H_AHEAD))
         miscp = ctx.enter_context(tc.psum_pool(name="miscp", bufs=1))
@@ -54,14 +52,13 @@ def tile_cin_pb_kernel(tc, h2, x0, W3, b3, out):
         ident_f = const.tile([P, P], F32, name="ident_f")
         sel = const.tile([P, NI, P], F32, name="sel")
         sel_bf = const.tile([P, H_AHEAD, P], BF16, name="sel_bf")
-        res = const.tile([P, 2, P], F32, name="res")
+        res = const.tile([P, P], F32, name="res")
         b3f = const.tile([P, 2], F32, name="b3f")
         junk = const.tile([P, ND], F32, name="junk")
-        o_sb = const.tile([NB, NC], F32, name="o_sb")
-        acc = [
-            [accp.tile([P, HALF], F32, name="acc%d%d" % (ct, h)) for h in range(2)]
-            for ct in range(2)
-        ]
+        o_sb = const.tile([P, P], F32, name="o_sb")
+        y0 = const.tile([P, 2, 16, ND], F32, name="y0")
+        acc_h0 = [accp.tile([P, HALF], F32, name="acc_h0_%d" % ct, tag="a%d" % ct) for ct in range(2)]
+        acc_q = {2: [accp.tile([P, QUART], F32, name="acc_q2_%d" % ct, tag="b%d" % ct) for ct in range(2)]}
 
         h2v = h2.rearrange("b f d -> f b d")
         xv = x0.rearrange("b (ga r) d -> ga b (r d)", ga=8)
@@ -118,7 +115,6 @@ def tile_cin_pb_kernel(tc, h2, x0, W3, b3, out):
             )
 
         hps_of = {}
-        hg_of = {}
 
         def spread_h(r):
             h, i = divmod(r, NI)
@@ -142,18 +138,6 @@ def tile_cin_pb_kernel(tc, h2, x0, W3, b3, out):
                     start=True,
                     stop=True,
                 )
-                hgps = miscp.tile([P, G_COLS], F32, name="hgps", tag="misc")
-                nc.tensor.matmul(
-                    out=hgps[:],
-                    lhsT=sel[:, i, :],
-                    rhs=h2d[:, (h + 1) * HALF - G_COLS : (h + 1) * HALF, :]
-                    .rearrange("p w e -> p (w e)")
-                    .bitcast(F32),
-                    start=True,
-                    stop=True,
-                )
-                hg_of[r] = hgp.tile([P, G_COLS], F32, name="hg")
-                nc.scalar.copy(out=hg_of[r][:], in_=hgps[:])
             hps_of[r] = hps
 
         zb_of = {}
@@ -163,22 +147,14 @@ def tile_cin_pb_kernel(tc, h2, x0, W3, b3, out):
             h = r // NI
             if r not in zb_of:
                 zb_of[r] = zbp.tile([P, NT, HALF * 4], BF16, name="zb", align_bytes=64)
-            if w0 + nw <= HALF:
-                engine = nc.vector
-                pairs = hps_of[r][:, w0 : w0 + nw]
-            else:
-                engine = nc.gpsimd
-                w0 = HALF - G_COLS
-                nw = G_COLS
-                pairs = hg_of[r][:]
-            engine.tensor_tensor(
+            nc.vector.tensor_tensor(
                 out=zb_of[r][:, t, w0 * 4 : (w0 + nw) * 4].rearrange(
                     "p (w a e) -> p w a e", a=2, e=2
                 ),
                 in0=xg[:, t, h * HALF + w0 : h * HALF + w0 + nw, :].rearrange(
                     "p w (a e) -> p w a e", a=2
                 ),
-                in1=pairs
+                in1=hps_of[r][:, w0 : w0 + nw]
                 .bitcast(BF16)
                 .rearrange("p (w e) -> p w e", e=2)
                 .unsqueeze(2)
@@ -186,44 +162,71 @@ def tile_cin_pb_kernel(tc, h2, x0, W3, b3, out):
                 op=MULT,
             )
 
-        def quantise_z(r, t0, nt):
+        def quantise_z(r, c0, ncol):
             if r not in zq_of:
                 zc = zcp.tile([P, NT * HALF], U32, name="zc", align_bytes=64)
                 zs = zcp.tile([P, NT * HALF], U8, name="zs", align_bytes=64)
                 zq_of[r] = (zc, zs)
             zc, zs = zq_of[r]
             nc.vector.quantize_mx(
-                out=zc[:, t0 * HALF : (t0 + nt) * HALF].bitcast(FP8X4),
-                scales=zs[:, t0 * HALF : (t0 + nt) * HALF],
-                in_=zb_of[r][:, t0 : t0 + nt, :].rearrange("p t w -> p (t w)"),
+                out=zc[:, c0 : c0 + ncol].bitcast(FP8X4),
+                scales=zs[:, c0 : c0 + ncol],
+                in_=zb_of[r][:].rearrange("p t w -> p (t w)")[:, 4 * c0 : 4 * (c0 + ncol)],
             )
 
-        def contract(r, t):
-            h, i = divmod(r, NI)
-            s = NT * i + t
+        def contract(r, t, w0, nw, group):
+            s = NT * (r % NI) + t
             zc, zs = zq_of[r]
             for ct in range(2):
                 nc.tensor.matmul_mx(
-                    out=acc[ct][h][:],
+                    out=group[ct][:],
                     lhsT=wc[:, s, ct * P : (ct + 1) * P].bitcast(FP8X4),
                     lhsT_scale=ws[:, s, ct * P : (ct + 1) * P],
-                    rhs=zc[:, t * HALF : (t + 1) * HALF].bitcast(FP8X4),
-                    rhs_scale=zs[:, t * HALF : (t + 1) * HALF],
+                    rhs=zc[:, t * HALF + w0 : t * HALF + w0 + nw].bitcast(FP8X4),
+                    rhs_scale=zs[:, t * HALF + w0 : t * HALF + w0 + nw],
                     start=(s == 0),
                     stop=(s == NI * NT - 1),
                 )
 
         def pool_first_half():
             for ct in range(2):
+                nc.scalar.activation(
+                    out=y0[:, ct, :, :].rearrange("p b d -> p (b d)"),
+                    in_=acc_h0[ct][:],
+                    func=RELU,
+                    bias=b3f[:, ct : ct + 1],
+                    scale=1.0,
+                )
+            acc_q[3] = [
+                accp.tile([P, QUART], F32, name="acc_q3_%d" % ct, tag="a%d" % ct) for ct in range(2)
+            ]
+
+        def sum_first_half():
+            for ct in range(2):
                 for b in range(16):
                     nc.scalar.activation(
                         out=junk[:],
-                        in_=acc[ct][0][:, b * ND : (b + 1) * ND],
+                        in_=y0[:, ct, b, :],
                         func=RELU,
-                        bias=b3f[:, ct : ct + 1],
-                        scale=1.0,
-                        accum_out=res[:, ct, b : b + 1],
+                        accum_out=res[:, ct * NB + b : ct * NB + b + 1],
                     )
+
+        def pool_quarter(q):
+            for ct in range(2):
+                y = epi.tile([P, 8, ND], F32, name="y")
+                nc.scalar.activation(
+                    out=y[:].rearrange("p b d -> p (b d)"),
+                    in_=acc_q[q][ct][:],
+                    func=RELU,
+                    bias=b3f[:, ct : ct + 1],
+                    scale=1.0,
+                )
+                nc.vector.tensor_reduce(
+                    out=res[:, ct * NB + 8 * q : ct * NB + 8 * q + 8],
+                    in_=y[:],
+                    axis=mybir.AxisListType.X,
+                    op=ADD,
+                )
 
         nc.scalar.dma_start(**load_h(0))
         load_x([nc.sync, nc.scalar], 0, 16, 0, 128)
@@ -263,6 +266,12 @@ def tile_cin_pb_kernel(tc, h2, x0, W3, b3, out):
         regroup_w(0)
         regroup_w(1)
         dup_h(nc.scalar.copy, HALF, HALF)
+        for i in range(2, 5):
+            regroup_w(i)
+        regroup_x(nc.scalar.copy, 0, 16, 16)
+        regroup_x(nc.scalar.copy, 1, 16, 16)
+        for i in range(5, NI):
+            regroup_w(i)
 
         regroup_x(nc.vector.tensor_copy, 0, 0, 8)
         for t in range(NT):
@@ -277,26 +286,14 @@ def tile_cin_pb_kernel(tc, h2, x0, W3, b3, out):
 
         contracted = 0
         w_done = 0
-        for r in range(N_PAIRS):
-            if r < 3:
-                regroup_w(r + 2)
-            elif r < 5:
-                regroup_x(nc.scalar.copy, r - 3, 16, 16)
-            elif r < 8:
-                regroup_w(r)
-            if r + H_AHEAD < N_PAIRS:
-                multiply(r + H_AHEAD, 1, HALF, 1)
-            if r == N_PAIRS - 1:
-                quantise_z(r, 0, 1)
-                quantise_z(r, 1, 1)
-            else:
-                quantise_z(r, 0, NT)
+        for r in range(N_PAIRS - 1):
+            quantise_z(r, 0, NT * HALF)
             if r >= 2 and r % 2 == 0 and w_done < NI:
                 quantise_w(w_done // 2)
                 w_done += 2
             if r + H_AHEAD < N_PAIRS:
-                multiply(r + H_AHEAD, 0, 0, HALF)
-                multiply(r + H_AHEAD, 1, 0, HALF - G_COLS)
+                for t in range(NT):
+                    multiply(r + H_AHEAD, t, 0, HALF)
                 if r + 2 * H_AHEAD < N_PAIRS:
                     spread_h(r + 2 * H_AHEAD)
             if r == 5:
@@ -305,27 +302,31 @@ def tile_cin_pb_kernel(tc, h2, x0, W3, b3, out):
                 nc.scalar.copy(out=b3f[:], in_=bps[:, 0:2])
             while contracted <= r and contracted % NI < w_done:
                 for t in range(NT):
-                    contract(contracted, t)
+                    if contracted < NI:
+                        contract(contracted, t, 0, HALF, acc_h0)
+                    else:
+                        for q in (2, 3):
+                            contract(contracted, t, (q - 2) * QUART, QUART, acc_q[q])
                 contracted += 1
                 if contracted == NI:
                     pool_first_half()
+                if contracted == NI + 1:
+                    sum_first_half()
 
+        r = N_PAIRS - 1
+        for q in (2, 3):
+            for t in range(NT):
+                quantise_z(r, t * HALF + (q - 2) * QUART, QUART)
+        for q in (2, 3):
+            for t in range(NT):
+                contract(r, t, (q - 2) * QUART, QUART, acc_q[q])
+        for q in (2, 3):
+            pool_quarter(q)
+
+        tps = miscp.tile([P, P], F32, name="tps", tag="misc")
+        nc.tensor.transpose(out=tps[:], in_=res[:], identity=ident_f[:])
+        nc.scalar.copy(out=o_sb[:], in_=tps[:])
         for ct in range(2):
-            y = epi.tile([P, 16, ND], F32, name="y")
-            nc.scalar.activation(
-                out=y[:].rearrange("p b d -> p (b d)"),
-                in_=acc[ct][1][:],
-                func=RELU,
-                bias=b3f[:, ct : ct + 1],
-                scale=1.0,
+            nc.sync.dma_start(
+                out=out[:, ct * P : (ct + 1) * P], in_=o_sb[ct * NB : (ct + 1) * NB, :]
             )
-            nc.vector.tensor_reduce(
-                out=res[:, ct, 16:32], in_=y[:], axis=mybir.AxisListType.X, op=ADD
-            )
-        tps = miscp.tile([P, 2 * P], F32, name="tps", tag="misc")
-        for ct in range(2):
-            nc.tensor.transpose(
-                out=tps[:, ct * P : (ct + 1) * P], in_=res[:, ct, :], identity=ident_f[:]
-            )
-        nc.scalar.copy(out=o_sb[:], in_=tps[0:NB, :])
-        nc.sync.dma_start(out=out[:, :], in_=o_sb[:])

@@ -23,6 +23,8 @@ HALF = 512
 QUART = 256
 N_PAIRS = 2 * NI
 H_AHEAD = 3
+GW = 64
+VW = HALF - GW
 
 FLOPS = 2 * NW * 8192 * NC
 
@@ -51,7 +53,8 @@ def tile_cin_pb_kernel(tc, h2, x0, W3, b3, out):
         ident_bf = const.tile([P, P], BF16, name="ident_bf")
         ident_f = const.tile([P, P], F32, name="ident_f")
         sel = const.tile([P, NI, P], F32, name="sel")
-        sel_bf = const.tile([P, H_AHEAD, P], BF16, name="sel_bf")
+        sel_bf = const.tile([P, NI, P], BF16, name="sel_bf")
+        hgs = const.tile([P, 2, NI, GW], BF16, name="hgs")
         res = const.tile([P, P], F32, name="res")
         b3f = const.tile([P, 2], F32, name="b3f")
         junk = const.tile([P, ND], F32, name="junk")
@@ -120,19 +123,19 @@ def tile_cin_pb_kernel(tc, h2, x0, W3, b3, out):
             h, i = divmod(r, NI)
             hps = hpsp.tile([P, HALF], F32, name="hps")
             if r < H_AHEAD:
-                for k in range(2):
+                for w0, w1 in ((0, QUART), (QUART, VW)):
                     nc.tensor.matmul(
-                        out=hps[:, k * QUART : (k + 1) * QUART].bitcast(BF16),
+                        out=hps[:, w0:w1].bitcast(BF16),
                         lhsT=sel_bf[:, i, :],
-                        rhs=h2d[:, k * QUART : (k + 1) * QUART, :].rearrange("p w e -> p (w e)"),
+                        rhs=h2d[:, w0:w1, :].rearrange("p w e -> p (w e)"),
                         start=True,
                         stop=True,
                     )
             else:
                 nc.tensor.matmul(
-                    out=hps[:],
+                    out=hps[:, 0:VW],
                     lhsT=sel[:, i, :],
-                    rhs=h2d[:, h * HALF : (h + 1) * HALF, :]
+                    rhs=h2d[:, h * HALF : h * HALF + VW, :]
                     .rearrange("p w e -> p (w e)")
                     .bitcast(F32),
                     start=True,
@@ -143,10 +146,30 @@ def tile_cin_pb_kernel(tc, h2, x0, W3, b3, out):
         zb_of = {}
         zq_of = {}
 
+        def spread_h_gp(h):
+            hgp = miscp.tile([P, NI, GW], BF16, name="hgp", tag="misc")
+            for i in range(NI):
+                nc.tensor.matmul(
+                    out=hgp[:, i, :],
+                    lhsT=sel_bf[:, i, :],
+                    rhs=h2t[:, h * HALF + VW : (h + 1) * HALF],
+                    start=True,
+                    stop=True,
+                )
+            return hgp
+
+        def multiply_gp(r):
+            h, i = divmod(r, NI)
+            zb_of[r] = zbp.tile([P, NT, HALF * 4], BF16, name="zb", align_bytes=64)
+            nc.gpsimd.tensor_tensor(
+                out=zb_of[r][:, :, VW * 4 : HALF * 4].rearrange("p t (w j) -> p t w j", j=4),
+                in0=xg[:, :, h * HALF + VW : (h + 1) * HALF, :],
+                in1=hgs[:, h, i, :].unsqueeze(1).unsqueeze(3).to_broadcast([P, NT, GW, 4]),
+                op=MULT,
+            )
+
         def multiply(r, t, w0, nw):
             h = r // NI
-            if r not in zb_of:
-                zb_of[r] = zbp.tile([P, NT, HALF * 4], BF16, name="zb", align_bytes=64)
             nc.vector.tensor_tensor(
                 out=zb_of[r][:, t, w0 * 4 : (w0 + nw) * 4].rearrange(
                     "p (w a e) -> p w a e", a=2, e=2
@@ -243,10 +266,10 @@ def tile_cin_pb_kernel(tc, h2, x0, W3, b3, out):
 
         nc.vector.tensor_copy(
             out=sel_bf[:].rearrange("p i (ph r) -> p i ph r", r=8),
-            in_=ident_bf[:, 0 : 16 * H_AHEAD]
-            .rearrange("p (i ph) -> p i ph", i=H_AHEAD)
+            in_=ident_bf[:]
+            .rearrange("p (i ph) -> p i ph", i=NI)
             .unsqueeze(3)
-            .to_broadcast([P, H_AHEAD, 16, 8]),
+            .to_broadcast([P, NI, 16, 8]),
         )
         nc.vector.tensor_copy(
             out=sel[:].rearrange("p i (ph r) -> p i ph r", r=8),
@@ -256,16 +279,20 @@ def tile_cin_pb_kernel(tc, h2, x0, W3, b3, out):
             .to_broadcast([P, NI, 16, 8]),
         )
         dup_h(nc.vector.tensor_copy, 0, QUART)
-        dup_h(nc.vector.tensor_copy, QUART, QUART)
+        dup_h(nc.vector.tensor_copy, QUART, VW - QUART)
         for r in range(H_AHEAD):
             spread_h(r)
+        hgp0 = spread_h_gp(0)
 
         regroup_x(nc.scalar.copy, 0, 8, 8)
+        nc.scalar.copy(out=hgs[:, 0, :, :], in_=hgp0[:])
         regroup_x(nc.scalar.copy, 1, 0, 8)
         regroup_x(nc.scalar.copy, 1, 8, 8)
         regroup_w(0)
         regroup_w(1)
-        dup_h(nc.scalar.copy, HALF, HALF)
+        dup_h(nc.scalar.copy, HALF, VW)
+        hgp1 = spread_h_gp(1)
+        nc.scalar.copy(out=hgs[:, 1, :, :], in_=hgp1[:])
         for i in range(2, 5):
             regroup_w(i)
         regroup_x(nc.scalar.copy, 0, 16, 16)
@@ -274,13 +301,15 @@ def tile_cin_pb_kernel(tc, h2, x0, W3, b3, out):
             regroup_w(i)
 
         regroup_x(nc.vector.tensor_copy, 0, 0, 8)
+        for r in range(H_AHEAD + 1):
+            multiply_gp(r)
         for t in range(NT):
             for r in range(H_AHEAD):
                 if r == 0:
                     multiply(r, t, 0, QUART)
-                    multiply(r, t, QUART, QUART)
+                    multiply(r, t, QUART, VW - QUART)
                 else:
-                    multiply(r, t, 0, HALF)
+                    multiply(r, t, 0, VW)
                 if t == NT - 1:
                     spread_h(r + H_AHEAD)
 
@@ -291,9 +320,11 @@ def tile_cin_pb_kernel(tc, h2, x0, W3, b3, out):
             if r >= 2 and r % 2 == 0 and w_done < NI:
                 quantise_w(w_done // 2)
                 w_done += 2
+            if r + H_AHEAD + 1 < N_PAIRS:
+                multiply_gp(r + H_AHEAD + 1)
             if r + H_AHEAD < N_PAIRS:
                 for t in range(NT):
-                    multiply(r + H_AHEAD, t, 0, HALF)
+                    multiply(r + H_AHEAD, t, 0, VW)
                 if r + 2 * H_AHEAD < N_PAIRS:
                     spread_h(r + 2 * H_AHEAD)
             if r == 5:

@@ -23,8 +23,9 @@ HALF = 512
 QUART = 256
 N_PAIRS = 2 * NI
 H_AHEAD = 3
-GW = 64
+GW = 96
 VW = HALF - GW
+G_LEAD = H_AHEAD + 1
 
 FLOPS = 2 * NW * 8192 * NC
 
@@ -35,7 +36,7 @@ def tile_cin_pb_kernel(tc, h2, x0, W3, b3, out):
         ctx.enter_context(tc.manual_schedule())
         const = ctx.enter_context(tc.tile_pool(name="const", bufs=1))
         wgp = ctx.enter_context(tc.tile_pool(name="wgp", bufs=NI // 2))
-        zbp = ctx.enter_context(tc.tile_pool(name="zbp", bufs=4))
+        zbp = ctx.enter_context(tc.tile_pool(name="zbp", bufs=G_LEAD))
         zcp = ctx.enter_context(tc.tile_pool(name="zcp", bufs=6))
         epi = ctx.enter_context(tc.tile_pool(name="epi", bufs=4))
         accp = ctx.enter_context(tc.psum_pool(name="accp", bufs=1))
@@ -75,7 +76,7 @@ def tile_cin_pb_kernel(tc, h2, x0, W3, b3, out):
 
         def load_x(queues, b0, nb, c0, ncol):
             for ga in range(8):
-                queues[ga % len(queues)].dma_start(
+                queues[ga].dma_start(
                     out=xraw[ga:P:8, b0 : b0 + nb, c0 : c0 + ncol],
                     in_=xv[ga : ga + 1, b0 : b0 + nb, c0 : c0 + ncol].to_broadcast(
                         [16, nb, ncol]
@@ -123,7 +124,7 @@ def tile_cin_pb_kernel(tc, h2, x0, W3, b3, out):
             h, i = divmod(r, NI)
             hps = hpsp.tile([P, HALF], F32, name="hps")
             if r < H_AHEAD:
-                for w0, w1 in ((0, QUART), (QUART, VW)):
+                for w0, w1 in ((GW, QUART), (QUART, HALF)):
                     nc.tensor.matmul(
                         out=hps[:, w0:w1].bitcast(BF16),
                         lhsT=sel_bf[:, i, :],
@@ -133,9 +134,9 @@ def tile_cin_pb_kernel(tc, h2, x0, W3, b3, out):
                     )
             else:
                 nc.tensor.matmul(
-                    out=hps[:, 0:VW],
+                    out=hps[:, GW:HALF],
                     lhsT=sel[:, i, :],
-                    rhs=h2d[:, h * HALF : h * HALF + VW, :]
+                    rhs=h2d[:, h * HALF + GW : (h + 1) * HALF, :]
                     .rearrange("p w e -> p (w e)")
                     .bitcast(F32),
                     start=True,
@@ -152,19 +153,20 @@ def tile_cin_pb_kernel(tc, h2, x0, W3, b3, out):
                 nc.tensor.matmul(
                     out=hgp[:, i, :],
                     lhsT=sel_bf[:, i, :],
-                    rhs=h2t[:, h * HALF + VW : (h + 1) * HALF],
+                    rhs=h2t[:, h * HALF : h * HALF + GW],
                     start=True,
                     stop=True,
                 )
             return hgp
 
-        def multiply_gp(r):
+        def multiply_gp(r, t0, nt):
             h, i = divmod(r, NI)
-            zb_of[r] = zbp.tile([P, NT, HALF * 4], BF16, name="zb", align_bytes=64)
+            if r not in zb_of:
+                zb_of[r] = zbp.tile([P, NT, HALF * 4], BF16, name="zb", align_bytes=64)
             nc.gpsimd.tensor_tensor(
-                out=zb_of[r][:, :, VW * 4 : HALF * 4].rearrange("p t (w j) -> p t w j", j=4),
-                in0=xg[:, :, h * HALF + VW : (h + 1) * HALF, :],
-                in1=hgs[:, h, i, :].unsqueeze(1).unsqueeze(3).to_broadcast([P, NT, GW, 4]),
+                out=zb_of[r][:, t0 : t0 + nt, 0 : GW * 4].rearrange("p t (w j) -> p t w j", j=4),
+                in0=xg[:, t0 : t0 + nt, h * HALF : h * HALF + GW, :],
+                in1=hgs[:, h, i, :].unsqueeze(1).unsqueeze(3).to_broadcast([P, nt, GW, 4]),
                 op=MULT,
             )
 
@@ -252,17 +254,18 @@ def tile_cin_pb_kernel(tc, h2, x0, W3, b3, out):
                 )
 
         nc.scalar.dma_start(**load_h(0))
-        load_x([nc.sync, nc.scalar], 0, 16, 0, 128)
-        load_x([nc.sync], 0, 16, 128, 128)
+        load_x([nc.sync, nc.scalar] * 3 + [nc.sync] * 2, 0, 16, 0, 128)
+        nc.gpsimd.memset(res[:], 0.0)
+        nc.scalar.copy(out=junk[:, 0:1], in_=res[:, 0:1])
+        load_x([nc.sync] * 8, 0, 16, 128, 128)
         nc.sync.dma_start(**load_h(1))
         for i in range(NI):
             nc.sync.dma_start(out=wraw[:, i, :], in_=wv[:, i, :])
         make_identity(nc, ident_bf[:])
         make_identity(nc, ident_f[:])
         nc.gpsimd.memset(bz[:], 0.0)
-        nc.gpsimd.memset(res[:], 0.0)
         nc.sync.dma_start(out=bz[0:2, :], in_=b3.rearrange("(ct c) -> ct c", ct=2))
-        load_x([nc.sync], 16, 16, 0, 256)
+        load_x([nc.sync] * 8, 16, 16, 0, 256)
 
         nc.vector.tensor_copy(
             out=sel_bf[:].rearrange("p i (ph r) -> p i ph r", r=8),
@@ -278,8 +281,8 @@ def tile_cin_pb_kernel(tc, h2, x0, W3, b3, out):
             .unsqueeze(3)
             .to_broadcast([P, NI, 16, 8]),
         )
-        dup_h(nc.vector.tensor_copy, 0, QUART)
-        dup_h(nc.vector.tensor_copy, QUART, VW - QUART)
+        dup_h(nc.vector.tensor_copy, GW, QUART - GW)
+        dup_h(nc.vector.tensor_copy, QUART, QUART)
         for r in range(H_AHEAD):
             spread_h(r)
         hgp0 = spread_h_gp(0)
@@ -290,7 +293,7 @@ def tile_cin_pb_kernel(tc, h2, x0, W3, b3, out):
         regroup_x(nc.scalar.copy, 1, 8, 8)
         regroup_w(0)
         regroup_w(1)
-        dup_h(nc.scalar.copy, HALF, VW)
+        dup_h(nc.scalar.copy, HALF + GW, VW)
         hgp1 = spread_h_gp(1)
         nc.scalar.copy(out=hgs[:, 1, :, :], in_=hgp1[:])
         for i in range(2, 5):
@@ -301,17 +304,18 @@ def tile_cin_pb_kernel(tc, h2, x0, W3, b3, out):
             regroup_w(i)
 
         regroup_x(nc.vector.tensor_copy, 0, 0, 8)
-        for r in range(H_AHEAD + 1):
-            multiply_gp(r)
         for t in range(NT):
             for r in range(H_AHEAD):
+                multiply_gp(r, t, 1)
                 if r == 0:
-                    multiply(r, t, 0, QUART)
-                    multiply(r, t, QUART, VW - QUART)
+                    multiply(r, t, GW, QUART - GW)
+                    multiply(r, t, QUART, QUART)
                 else:
-                    multiply(r, t, 0, VW)
+                    multiply(r, t, GW, VW)
                 if t == NT - 1:
                     spread_h(r + H_AHEAD)
+        for r in range(H_AHEAD, G_LEAD):
+            multiply_gp(r, 0, NT)
 
         contracted = 0
         w_done = 0
@@ -320,11 +324,11 @@ def tile_cin_pb_kernel(tc, h2, x0, W3, b3, out):
             if r >= 2 and r % 2 == 0 and w_done < NI:
                 quantise_w(w_done // 2)
                 w_done += 2
-            if r + H_AHEAD + 1 < N_PAIRS:
-                multiply_gp(r + H_AHEAD + 1)
+            if r + G_LEAD < N_PAIRS:
+                multiply_gp(r + G_LEAD, 0, NT)
             if r + H_AHEAD < N_PAIRS:
                 for t in range(NT):
-                    multiply(r + H_AHEAD, t, 0, VW)
+                    multiply(r + H_AHEAD, t, GW, VW)
                 if r + 2 * H_AHEAD < N_PAIRS:
                     spread_h(r + 2 * H_AHEAD)
             if r == 5:

@@ -23,7 +23,7 @@ HALF = 512
 QUART = 256
 N_PAIRS = 2 * NI
 H_AHEAD = 3
-GW = 96
+GW = 48
 VW = HALF - GW
 G_LEAD = H_AHEAD + 1
 

@@ -23,7 +23,7 @@ HALF = 512
 QUART = 256
 N_PAIRS = 2 * NI
 H_AHEAD = 3
-GW = 48
+GW = 64
 VW = HALF - GW
 G_LEAD = H_AHEAD + 1
 

@@ -26,6 +26,8 @@ H_AHEAD = 3
 GW = 64
 VW = HALF - GW
 G_LEAD = H_AHEAD + 1
+BF_FROM = 9
+W_ROUNDS = (2, 4, 6, 7)
 
 FLOPS = 2 * NW * 8192 * NC
 
@@ -123,12 +125,12 @@ def tile_cin_pb_kernel(tc, h2, x0, W3, b3, out):
         def spread_h(r):
             h, i = divmod(r, NI)
             hps = hpsp.tile([P, HALF], F32, name="hps")
-            if r < H_AHEAD:
+            if r < H_AHEAD or r >= BF_FROM:
                 for w0, w1 in ((GW, QUART), (QUART, HALF)):
                     nc.tensor.matmul(
                         out=hps[:, w0:w1].bitcast(BF16),
                         lhsT=sel_bf[:, i, :],
-                        rhs=h2d[:, w0:w1, :].rearrange("p w e -> p (w e)"),
+                        rhs=h2d[:, h * HALF + w0 : h * HALF + w1, :].rearrange("p w e -> p (w e)"),
                         start=True,
                         stop=True,
                     )
@@ -321,7 +323,7 @@ def tile_cin_pb_kernel(tc, h2, x0, W3, b3, out):
         w_done = 0
         for r in range(N_PAIRS - 1):
             quantise_z(r, 0, NT * HALF)
-            if r >= 2 and r % 2 == 0 and w_done < NI:
+            if r in W_ROUNDS:
                 quantise_w(w_done // 2)
                 w_done += 2
             if r + G_LEAD < N_PAIRS:

@@ -11,6 +11,7 @@ U8 = mybir.dt.uint8
 MULT = mybir.AluOpType.mult
 ADD = mybir.AluOpType.add
 RELU = mybir.ActivationFunctionType.Relu
+COPY = mybir.ActivationFunctionType.Copy
 
 P = 128
 NB = 32
@@ -23,11 +24,14 @@ HALF = 512
 QUART = 256
 N_PAIRS = 2 * NI
 H_AHEAD = 3
-GW = 64
-VW = HALF - GW
+G_COLS = 56
+G_COLS_S = 32
 G_LEAD = H_AHEAD + 1
-BF_FROM = 9
+S_PAIRS = range(9, N_PAIRS)
 W_ROUNDS = (2, 4, 6, 7)
+POOL_ROUND = 9
+SUM_ROUNDS = (10, 11)
+S_COLS = P
 
 FLOPS = 2 * NW * 8192 * NC
 
@@ -40,6 +44,7 @@ def tile_cin_pb_kernel(tc, h2, x0, W3, b3, out):
         wgp = ctx.enter_context(tc.tile_pool(name="wgp", bufs=NI // 2))
         zbp = ctx.enter_context(tc.tile_pool(name="zbp", bufs=G_LEAD))
         zcp = ctx.enter_context(tc.tile_pool(name="zcp", bufs=6))
+        ztp = ctx.enter_context(tc.tile_pool(name="ztp", bufs=2))
         epi = ctx.enter_context(tc.tile_pool(name="epi", bufs=4))
         accp = ctx.enter_context(tc.psum_pool(name="accp", bufs=1))
         hpsp = ctx.enter_context(tc.psum_pool(name="hpsp", bufs=H_AHEAD))
@@ -57,12 +62,16 @@ def tile_cin_pb_kernel(tc, h2, x0, W3, b3, out):
         ident_f = const.tile([P, P], F32, name="ident_f")
         sel = const.tile([P, NI, P], F32, name="sel")
         sel_bf = const.tile([P, NI, P], BF16, name="sel_bf")
-        hgs = const.tile([P, 2, NI, GW], BF16, name="hgs")
+        hgs = const.tile([P, 2, NI, G_COLS], BF16, name="hgs")
+        xn = const.tile([P, P], BF16, name="xn")
+        xt = const.tile([P, 2 * NT, 8, 2], BF16, name="xt")
+        ht = const.tile([P, P], F32, name="ht")
         res = const.tile([P, P], F32, name="res")
         b3f = const.tile([P, 2], F32, name="b3f")
         junk = const.tile([P, ND], F32, name="junk")
         o_sb = const.tile([P, P], F32, name="o_sb")
         y0 = const.tile([P, 2, 16, ND], F32, name="y0")
+        y1 = const.tile([P, 2, 16, ND // 2], F32, name="y1")
         acc_h0 = [accp.tile([P, HALF], F32, name="acc_h0_%d" % ct, tag="a%d" % ct) for ct in range(2)]
         acc_q = {2: [accp.tile([P, QUART], F32, name="acc_q2_%d" % ct, tag="b%d" % ct) for ct in range(2)]}
 
@@ -122,11 +131,18 @@ def tile_cin_pb_kernel(tc, h2, x0, W3, b3, out):
 
         hps_of = {}
 
+        def gpsimd_cols(r):
+            return G_COLS_S if r in S_PAIRS or r - 1 in S_PAIRS else G_COLS
+
+        def vector_cols(r):
+            return gpsimd_cols(r), HALF - S_COLS if r in S_PAIRS else HALF
+
         def spread_h(r):
             h, i = divmod(r, NI)
+            v0, v1 = vector_cols(r)
             hps = hpsp.tile([P, HALF], F32, name="hps")
-            if r < H_AHEAD or r >= BF_FROM:
-                for w0, w1 in ((GW, QUART), (QUART, HALF)):
+            if r < H_AHEAD or r in S_PAIRS:
+                for w0, w1 in ((v0, QUART), (QUART, v1)):
                     nc.tensor.matmul(
                         out=hps[:, w0:w1].bitcast(BF16),
                         lhsT=sel_bf[:, i, :],
@@ -136,9 +152,9 @@ def tile_cin_pb_kernel(tc, h2, x0, W3, b3, out):
                     )
             else:
                 nc.tensor.matmul(
-                    out=hps[:, GW:HALF],
+                    out=hps[:, v0:v1],
                     lhsT=sel[:, i, :],
-                    rhs=h2d[:, h * HALF + GW : (h + 1) * HALF, :]
+                    rhs=h2d[:, h * HALF + v0 : h * HALF + v1, :]
                     .rearrange("p w e -> p (w e)")
                     .bitcast(F32),
                     start=True,
@@ -150,12 +166,12 @@ def tile_cin_pb_kernel(tc, h2, x0, W3, b3, out):
         zq_of = {}
 
         def spread_h_gp(h):
-            hgp = miscp.tile([P, NI, GW], BF16, name="hgp", tag="misc")
+            hgp = miscp.tile([P, NI, G_COLS], BF16, name="hgp", tag="misc")
             for i in range(NI):
                 nc.tensor.matmul(
                     out=hgp[:, i, :],
                     lhsT=sel_bf[:, i, :],
-                    rhs=h2t[:, h * HALF : h * HALF + GW],
+                    rhs=h2t[:, h * HALF : h * HALF + G_COLS],
                     start=True,
                     stop=True,
                 )
@@ -163,13 +179,43 @@ def tile_cin_pb_kernel(tc, h2, x0, W3, b3, out):
 
         def multiply_gp(r, t0, nt):
             h, i = divmod(r, NI)
+            gw = gpsimd_cols(r)
             if r not in zb_of:
                 zb_of[r] = zbp.tile([P, NT, HALF * 4], BF16, name="zb", align_bytes=64)
             nc.gpsimd.tensor_tensor(
-                out=zb_of[r][:, t0 : t0 + nt, 0 : GW * 4].rearrange("p t (w j) -> p t w j", j=4),
-                in0=xg[:, t0 : t0 + nt, h * HALF : h * HALF + GW, :],
-                in1=hgs[:, h, i, :].unsqueeze(1).unsqueeze(3).to_broadcast([P, nt, GW, 4]),
+                out=zb_of[r][:, t0 : t0 + nt, 0 : gw * 4].rearrange("p t (w j) -> p t w j", j=4),
+                in0=xg[:, t0 : t0 + nt, h * HALF : h * HALF + gw, :],
+                in1=hgs[:, h, i, 0:gw].unsqueeze(1).unsqueeze(3).to_broadcast([P, nt, gw, 4]),
                 op=MULT,
+            )
+
+        zt_of = {}
+
+        def scale_rows(r):
+            i = r % NI
+            zt_of[r] = ztp.tile([P, 2 * NT, 16, 16], BF16, name="zt")
+            for f in range(16):
+                nc.scalar.activation(
+                    out=zt_of[r][:, :, f, :],
+                    in_=xt[:].rearrange("p s g e -> p s (g e)"),
+                    func=COPY,
+                    scale=ht[:, 16 * i + f : 16 * i + f + 1],
+                )
+
+        def turn_rows(r):
+            zp = miscp.tile([P, 2 * NT, P], F32, name="zp", tag="misc")
+            for s in range(2 * NT):
+                nc.tensor.transpose(
+                    out=zp[:, s, :],
+                    in_=zt_of[r][:, s, :, :].rearrange("p f g -> p (f g)").bitcast(F32),
+                    identity=ident_f[:],
+                )
+            nc.scalar.copy(
+                out=zb_of[r][:]
+                .rearrange("p t w -> p (t w)")
+                .bitcast(F32)
+                .rearrange("p (t w a) -> p t w a", t=NT, a=2)[:, :, HALF - S_COLS :, :],
+                in_=zp[:].rearrange("p (t a) n -> p t n a", t=NT),
             )
 
         def multiply(r, t, w0, nw):
@@ -228,15 +274,25 @@ def tile_cin_pb_kernel(tc, h2, x0, W3, b3, out):
                 accp.tile([P, QUART], F32, name="acc_q3_%d" % ct, tag="a%d" % ct) for ct in range(2)
             ]
 
-        def sum_first_half():
+        def fold(out, in_):
+            n = in_.shape[-1] // 2
+            nc.gpsimd.tensor_tensor(out=out, in0=in_[:, :, 0:n], in1=in_[:, :, n : 2 * n], op=ADD)
+
+        def sum_first_half_begin(ct):
+            fold(y1[:, ct, :, :], y0[:, ct, :, :])
+
+        def sum_first_half_end():
+            tail = zbp.tile([P, NT, HALF * 4], BF16, name="zb", align_bytes=64)
+            words = tail[:].rearrange("p t w -> p (t w)").bitcast(F32)
+            part, at = y1[:].rearrange("p ct b d -> p (ct b) d"), 0
+            for n in (8, 4, 2):
+                nxt = words[:, at : at + 2 * 16 * n].rearrange("p (s d) -> p s d", d=n)
+                fold(nxt, part)
+                part, at = nxt, at + 2 * 16 * n
             for ct in range(2):
-                for b in range(16):
-                    nc.scalar.activation(
-                        out=junk[:],
-                        in_=y0[:, ct, b, :],
-                        func=RELU,
-                        accum_out=res[:, ct * NB + b : ct * NB + b + 1],
-                    )
+                fold(
+                    res[:, ct * NB : ct * NB + 16].unsqueeze(2), part[:, 16 * ct : 16 * ct + 16, :]
+                )
 
         def pool_quarter(q):
             for ct in range(2):
@@ -261,6 +317,11 @@ def tile_cin_pb_kernel(tc, h2, x0, W3, b3, out):
         nc.scalar.copy(out=junk[:, 0:1], in_=res[:, 0:1])
         load_x([nc.sync] * 8, 0, 16, 128, 128)
         nc.sync.dma_start(**load_h(1))
+        for k in range(2):
+            nc.sync.dma_start(
+                out=xn[64 * k : 64 * k + 64, :].rearrange("p (b d) -> p b d", d=ND),
+                in_=x0[NB - 4 - 4 * k : NB - 4 * k, :, :].rearrange("b g d -> g b d"),
+            )
         for i in range(NI):
             nc.sync.dma_start(out=wraw[:, i, :], in_=wv[:, i, :])
         make_identity(nc, ident_bf[:])
@@ -283,7 +344,7 @@ def tile_cin_pb_kernel(tc, h2, x0, W3, b3, out):
             .unsqueeze(3)
             .to_broadcast([P, NI, 16, 8]),
         )
-        dup_h(nc.vector.tensor_copy, GW, QUART - GW)
+        dup_h(nc.vector.tensor_copy, G_COLS, QUART - G_COLS)
         dup_h(nc.vector.tensor_copy, QUART, QUART)
         for r in range(H_AHEAD):
             spread_h(r)
@@ -295,14 +356,10 @@ def tile_cin_pb_kernel(tc, h2, x0, W3, b3, out):
         regroup_x(nc.scalar.copy, 1, 8, 8)
         regroup_w(0)
         regroup_w(1)
-        dup_h(nc.scalar.copy, HALF + GW, VW)
+        dup_h(nc.scalar.copy, HALF, HALF)
         hgp1 = spread_h_gp(1)
         nc.scalar.copy(out=hgs[:, 1, :, :], in_=hgp1[:])
         for i in range(2, 5):
-            regroup_w(i)
-        regroup_x(nc.scalar.copy, 0, 16, 16)
-        regroup_x(nc.scalar.copy, 1, 16, 16)
-        for i in range(5, NI):
             regroup_w(i)
 
         regroup_x(nc.vector.tensor_copy, 0, 0, 8)
@@ -310,10 +367,10 @@ def tile_cin_pb_kernel(tc, h2, x0, W3, b3, out):
             for r in range(H_AHEAD):
                 multiply_gp(r, t, 1)
                 if r == 0:
-                    multiply(r, t, GW, QUART - GW)
+                    multiply(r, t, G_COLS, QUART - G_COLS)
                     multiply(r, t, QUART, QUART)
                 else:
-                    multiply(r, t, GW, VW)
+                    multiply(r, t, G_COLS, HALF - G_COLS)
                 if t == NT - 1:
                     spread_h(r + H_AHEAD)
         for r in range(H_AHEAD, G_LEAD):
@@ -322,22 +379,39 @@ def tile_cin_pb_kernel(tc, h2, x0, W3, b3, out):
         contracted = 0
         w_done = 0
         for r in range(N_PAIRS - 1):
-            quantise_z(r, 0, NT * HALF)
+            if r < N_PAIRS - 2:
+                quantise_z(r, 0, NT * HALF)
+            else:
+                for t in range(NT):
+                    quantise_z(r, t * HALF, HALF)
             if r in W_ROUNDS:
                 quantise_w(w_done // 2)
                 w_done += 2
             if r + G_LEAD < N_PAIRS:
                 multiply_gp(r + G_LEAD, 0, NT)
-            if r + H_AHEAD < N_PAIRS:
+            if r == 1:
+                turned = miscp.tile([P, 2, P], BF16, name="turned", tag="misc")
+                for k, src in enumerate((xn[:], h2t[:, NW - S_COLS :])):
+                    nc.tensor.transpose(out=turned[:, k, :], in_=src, identity=ident_bf[:])
+                nc.scalar.copy(
+                    out=xt[:], in_=turned[:, 0, 0:64].rearrange("p (g s e) -> p s g e", g=8, e=2)
+                )
+                nc.scalar.copy(out=ht[:], in_=turned[:, 1, :])
                 for t in range(NT):
-                    multiply(r + H_AHEAD, t, GW, VW)
-                if r + 2 * H_AHEAD < N_PAIRS:
-                    spread_h(r + 2 * H_AHEAD)
-            if r == 5:
-                bps = miscp.tile([P, P], BF16, name="bps", tag="misc")
-                nc.tensor.transpose(out=bps[:], in_=bz[:], identity=ident_bf[:])
-                nc.scalar.copy(out=b3f[:], in_=bps[:, 0:2])
-            while contracted <= r and contracted % NI < w_done:
+                    regroup_x(nc.scalar.copy, t, 16, 16)
+                for i in range(5, NI):
+                    regroup_w(i)
+                scale_rows(S_PAIRS[0])
+            if r + 2 in S_PAIRS[:-1]:
+                scale_rows(r + 3)
+                turn_rows(r + 2)
+            if r == POOL_ROUND:
+                pool_first_half()
+            if r in SUM_ROUNDS:
+                sum_first_half_begin(SUM_ROUNDS.index(r))
+            if r == SUM_ROUNDS[-1] + 1:
+                sum_first_half_end()
+            while contracted <= r and contracted % NI < w_done and (contracted < NI or r >= POOL_ROUND):
                 for t in range(NT):
                     if contracted < NI:
                         contract(contracted, t, 0, HALF, acc_h0)
@@ -345,10 +419,18 @@ def tile_cin_pb_kernel(tc, h2, x0, W3, b3, out):
                         for q in (2, 3):
                             contract(contracted, t, (q - 2) * QUART, QUART, acc_q[q])
                 contracted += 1
-                if contracted == NI:
-                    pool_first_half()
-                if contracted == NI + 1:
-                    sum_first_half()
+            if r + 3 == S_PAIRS[-1]:
+                turn_rows(r + 3)
+            if r + H_AHEAD < N_PAIRS:
+                v0, v1 = vector_cols(r + H_AHEAD)
+                for t in range(NT):
+                    multiply(r + H_AHEAD, t, v0, v1 - v0)
+                if r + 2 * H_AHEAD < N_PAIRS:
+                    spread_h(r + 2 * H_AHEAD)
+            if r == 5:
+                bps = miscp.tile([P, P], BF16, name="bps", tag="misc")
+                nc.tensor.transpose(out=bps[:], in_=bz[:], identity=ident_bf[:])
+                nc.scalar.copy(out=b3f[:], in_=bps[:, 0:2])
 
         r = N_PAIRS - 1
         for q in (2, 3):

@@ -27,7 +27,7 @@ H_AHEAD = 3
 G_COLS = 56
 G_COLS_S = 32
 G_LEAD = H_AHEAD + 1
-S_PAIRS = range(9, N_PAIRS)
+S_PAIRS = range(NI, N_PAIRS)
 W_ROUNDS = (2, 4, 6, 7)
 POOL_ROUND = 9
 SUM_ROUNDS = (10, 11)
@@ -328,7 +328,7 @@ def tile_cin_pb_kernel(tc, h2, x0, W3, b3, out):
         make_identity(nc, ident_f[:])
         nc.gpsimd.memset(bz[:], 0.0)
         nc.sync.dma_start(out=bz[0:2, :], in_=b3.rearrange("(ct c) -> ct c", ct=2))
-        load_x([nc.sync] * 8, 16, 16, 0, 256)
+        load_x([nc.sync] * 8, 16, 16 - S_COLS // ND, 0, 256)
 
         nc.vector.tensor_copy(
             out=sel_bf[:].rearrange("p i (ph r) -> p i ph r", r=8),
@@ -356,10 +356,10 @@ def tile_cin_pb_kernel(tc, h2, x0, W3, b3, out):
         regroup_x(nc.scalar.copy, 1, 8, 8)
         regroup_w(0)
         regroup_w(1)
-        dup_h(nc.scalar.copy, HALF, HALF)
+        dup_h(nc.scalar.copy, HALF + G_COLS_S, HALF - S_COLS - G_COLS_S)
         hgp1 = spread_h_gp(1)
         nc.scalar.copy(out=hgs[:, 1, :, :], in_=hgp1[:])
-        for i in range(2, 5):
+        for i in range(2, 4):
             regroup_w(i)
 
         regroup_x(nc.vector.tensor_copy, 0, 0, 8)
@@ -379,7 +379,7 @@ def tile_cin_pb_kernel(tc, h2, x0, W3, b3, out):
         contracted = 0
         w_done = 0
         for r in range(N_PAIRS - 1):
-            if r < N_PAIRS - 2:
+            if r < N_PAIRS - 3:
                 quantise_z(r, 0, NT * HALF)
             else:
                 for t in range(NT):
@@ -398,8 +398,8 @@ def tile_cin_pb_kernel(tc, h2, x0, W3, b3, out):
                 )
                 nc.scalar.copy(out=ht[:], in_=turned[:, 1, :])
                 for t in range(NT):
-                    regroup_x(nc.scalar.copy, t, 16, 16)
-                for i in range(5, NI):
+                    regroup_x(nc.scalar.copy, t, 16, 16 - S_COLS // ND)
+                for i in range(4, NI):
                     regroup_w(i)
                 scale_rows(S_PAIRS[0])
             if r + 2 in S_PAIRS[:-1]:
@@ -446,6 +446,6 @@ def tile_cin_pb_kernel(tc, h2, x0, W3, b3, out):
         nc.tensor.transpose(out=tps[:], in_=res[:], identity=ident_f[:])
         nc.scalar.copy(out=o_sb[:], in_=tps[:])
         for ct in range(2):
-            nc.sync.dma_start(
+            (nc.sync, nc.scalar)[ct].dma_start(
                 out=out[:, ct * P : (ct + 1) * P], in_=o_sb[ct * NB : (ct + 1) * NB, :]
             )

@@ -29,7 +29,7 @@ G_COLS_S = 32
 G_LEAD = H_AHEAD + 1
 S_PAIRS = range(NI, N_PAIRS)
 W_ROUNDS = (2, 4, 6, 7)
-POOL_ROUND = 9
+POOL_ROUND = 8
 SUM_ROUNDS = (10, 11)
 S_COLS = P
 
@@ -390,13 +390,14 @@ def tile_cin_pb_kernel(tc, h2, x0, W3, b3, out):
             if r + G_LEAD < N_PAIRS:
                 multiply_gp(r + G_LEAD, 0, NT)
             if r == 1:
-                turned = miscp.tile([P, 2, P], BF16, name="turned", tag="misc")
-                for k, src in enumerate((xn[:], h2t[:, NW - S_COLS :])):
+                turned = miscp.tile([P, 3, P], BF16, name="turned", tag="misc")
+                for k, src in enumerate((xn[:], h2t[:, NW - S_COLS :], bz[:])):
                     nc.tensor.transpose(out=turned[:, k, :], in_=src, identity=ident_bf[:])
                 nc.scalar.copy(
                     out=xt[:], in_=turned[:, 0, 0:64].rearrange("p (g s e) -> p s g e", g=8, e=2)
                 )
                 nc.scalar.copy(out=ht[:], in_=turned[:, 1, :])
+                nc.scalar.copy(out=b3f[:], in_=turned[:, 2, 0:2])
                 for t in range(NT):
                     regroup_x(nc.scalar.copy, t, 16, 16 - S_COLS // ND)
                 for i in range(4, NI):
@@ -404,6 +405,7 @@ def tile_cin_pb_kernel(tc, h2, x0, W3, b3, out):
                 scale_rows(S_PAIRS[0])
             if r + 2 in S_PAIRS[:-1]:
                 scale_rows(r + 3)
+            if r + 2 in S_PAIRS[1:-1]:
                 turn_rows(r + 2)
             if r == POOL_ROUND:
                 pool_first_half()
@@ -427,10 +429,8 @@ def tile_cin_pb_kernel(tc, h2, x0, W3, b3, out):
                     multiply(r + H_AHEAD, t, v0, v1 - v0)
                 if r + 2 * H_AHEAD < N_PAIRS:
                     spread_h(r + 2 * H_AHEAD)
-            if r == 5:
-                bps = miscp.tile([P, P], BF16, name="bps", tag="misc")
-                nc.tensor.transpose(out=bps[:], in_=bz[:], identity=ident_bf[:])
-                nc.scalar.copy(out=b3f[:], in_=bps[:, 0:2])
+            if r + 2 == S_PAIRS[0]:
+                turn_rows(r + 2)
 
         r = N_PAIRS - 1
         for q in (2, 3):
@@ -446,6 +446,6 @@ def tile_cin_pb_kernel(tc, h2, x0, W3, b3, out):
         nc.tensor.transpose(out=tps[:], in_=res[:], identity=ident_f[:])
         nc.scalar.copy(out=o_sb[:], in_=tps[:])
         for ct in range(2):
-            (nc.sync, nc.scalar)[ct].dma_start(
+            nc.sync.dma_start(
                 out=out[:, ct * P : (ct + 1) * P], in_=o_sb[ct * NB : (ct + 1) * NB, :]
             )

from contextlib import ExitStack

import concourse.mybir as mybir
from concourse.masks import make_identity

FP8X4 = mybir.dt.float8_e4m3fn_x4
BF16 = mybir.dt.bfloat16
F32 = mybir.dt.float32
U32 = mybir.dt.uint32
U8 = mybir.dt.uint8
MULT = mybir.AluOpType.mult
ADD = mybir.AluOpType.add
RELU = mybir.ActivationFunctionType.Relu
COPY = mybir.ActivationFunctionType.Copy

P = 128
NB = 32
ND = 32
NW = NB * ND
NC = 256
NI = 8
NT = 2
HALF = 512
QUART = 256
N_PAIRS = 2 * NI
H_AHEAD = 3
G_COLS = 56
G_COLS_S = 32
G_LEAD = H_AHEAD + 1
S_PAIRS = range(NI, N_PAIRS)
W_ROUNDS = (2, 4, 6, 7)
POOL_ROUND = 8
SUM_ROUNDS = (10, 11)
S_COLS = P

FLOPS = 2 * NW * 8192 * NC


def tile_cin_pb_kernel(tc, h2, x0, W3, b3, out):
    nc = tc.nc
    with ExitStack() as ctx:
        ctx.enter_context(tc.manual_schedule())
        const = ctx.enter_context(tc.tile_pool(name="const", bufs=1))
        wgp = ctx.enter_context(tc.tile_pool(name="wgp", bufs=NI // 2))
        zbp = ctx.enter_context(tc.tile_pool(name="zbp", bufs=G_LEAD))
        zcp = ctx.enter_context(tc.tile_pool(name="zcp", bufs=6))
        ztp = ctx.enter_context(tc.tile_pool(name="ztp", bufs=2))
        epi = ctx.enter_context(tc.tile_pool(name="epi", bufs=4))
        accp = ctx.enter_context(tc.psum_pool(name="accp", bufs=1))
        hpsp = ctx.enter_context(tc.psum_pool(name="hpsp", bufs=H_AHEAD))
        miscp = ctx.enter_context(tc.psum_pool(name="miscp", bufs=1))

        h2t = const.tile([P, NW], BF16, name="h2t")
        h2d = const.tile([P, NW, 2], BF16, name="h2d")
        xraw = const.tile([P, NB, 256], BF16, name="xraw")
        wraw = const.tile([P, NI, 2048], BF16, name="wraw")
        bz = const.tile([P, P], BF16, name="bz")
        xg = const.tile([P, NT, NW, 4], BF16, name="xg")
        wc = const.tile([P, NI * NT, NC], U32, name="wc", align_bytes=64)
        ws = const.tile([P, NI * NT, NC], U8, name="ws", align_bytes=64)
        ident_bf = const.tile([P, P], BF16, name="ident_bf")
        ident_f = const.tile([P, P], F32, name="ident_f")
        sel = const.tile([P, NI, P], F32, name="sel")
        sel_bf = const.tile([P, NI, P], BF16, name="sel_bf")
        hgs = const.tile([P, 2, NI, G_COLS], BF16, name="hgs")
        xn = const.tile([P, P], BF16, name="xn")
        xt = const.tile([P, 2 * NT, 8, 2], BF16, name="xt")
        ht = const.tile([P, P], F32, name="ht")
        res = const.tile([P, P], F32, name="res")
        b3f = const.tile([P, 2], F32, name="b3f")
        junk = const.tile([P, ND], F32, name="junk")
        o_sb = const.tile([P, P], F32, name="o_sb")
        y0 = const.tile([P, 2, 16, ND], F32, name="y0")
        y1 = const.tile([P, 2, 16, ND // 2], F32, name="y1")
        acc_h0 = [accp.tile([P, HALF], F32, name="acc_h0_%d" % ct, tag="a%d" % ct) for ct in range(2)]
        acc_q = {2: [accp.tile([P, QUART], F32, name="acc_q2_%d" % ct, tag="b%d" % ct) for ct in range(2)]}

        h2v = h2.rearrange("b f d -> f b d")
        xv = x0.rearrange("b (ga r) d -> ga b (r d)", ga=8)
        wv = W3.rearrange("(i p r) c -> p i (r c)", i=NI, p=P, r=8)

        def load_h(h):
            return dict(
                out=h2t[:, h * HALF : (h + 1) * HALF].rearrange("p (b d) -> p b d", d=ND),
                in_=h2v[:, 16 * h : 16 * h + 16, :],
            )

        def load_x(queues, b0, nb, c0, ncol):
            for ga in range(8):
                queues[ga].dma_start(
                    out=xraw[ga:P:8, b0 : b0 + nb, c0 : c0 + ncol],
                    in_=xv[ga : ga + 1, b0 : b0 + nb, c0 : c0 + ncol].to_broadcast(
                        [16, nb, ncol]
                    ),
                )

        def dup_h(copy, w0, nw):
            copy(
                out=h2d[:, w0 : w0 + nw, :],
                in_=h2t[:, w0 : w0 + nw].unsqueeze(2).to_broadcast([P, nw, 2]),
            )

        def regroup_x(copy, t, b0, nb):
            copy(
                out=xg[:, t, b0 * ND : (b0 + nb) * ND, :].rearrange("p (b d) j -> p b d j", d=ND),
                in_=xraw[:, b0 : b0 + nb, t * 128 : (t + 1) * 128].rearrange(
                    "p b (j d) -> p b d j", j=4
                ),
            )

        wg_of = {}

        def regroup_w(i):
            if i // 2 not in wg_of:
                wg_of[i // 2] = wgp.tile([P, 2 * NT, NC, 4], BF16, name="wg", align_bytes=64)
            wg = wg_of[i // 2]
            for t in range(NT):
                nc.scalar.copy(
                    out=wg[:, NT * (i % 2) + t, :, :].rearrange("p (c q) j -> p c j q", q=4),
                    in_=wraw[:, i, t * 1024 : (t + 1) * 1024].rearrange(
                        "p (j c q) -> p c j q", j=4, q=4
                    ),
                )

        def quantise_w(ii):
            nc.vector.quantize_mx(
                out=wc[:, 4 * ii : 4 * ii + 4, :].rearrange("p s c -> p (s c)").bitcast(FP8X4),
                scales=ws[:, 4 * ii : 4 * ii + 4, :].rearrange("p s c -> p (s c)"),
                in_=wg_of[ii][:].rearrange("p s c j -> p (s c j)"),
            )

        hps_of = {}

        def gpsimd_cols(r):
            return G_COLS_S if r in S_PAIRS or r - 1 in S_PAIRS else G_COLS

        def vector_cols(r):
            return gpsimd_cols(r), HALF - S_COLS if r in S_PAIRS else HALF

        def spread_h(r):
            h, i = divmod(r, NI)
            v0, v1 = vector_cols(r)
            hps = hpsp.tile([P, HALF], F32, name="hps")
            if r < H_AHEAD or r in S_PAIRS:
                for w0, w1 in ((v0, QUART), (QUART, v1)):
                    nc.tensor.matmul(
                        out=hps[:, w0:w1].bitcast(BF16),
                        lhsT=sel_bf[:, i, :],
                        rhs=h2d[:, h * HALF + w0 : h * HALF + w1, :].rearrange("p w e -> p (w e)"),
                        start=True,
                        stop=True,
                    )
            else:
                nc.tensor.matmul(
                    out=hps[:, v0:v1],
                    lhsT=sel[:, i, :],
                    rhs=h2d[:, h * HALF + v0 : h * HALF + v1, :]
                    .rearrange("p w e -> p (w e)")
                    .bitcast(F32),
                    start=True,
                    stop=True,
                )
            hps_of[r] = hps

        zb_of = {}
        zq_of = {}

        def spread_h_gp(h):
            hgp = miscp.tile([P, NI, G_COLS], BF16, name="hgp", tag="misc")
            for i in range(NI):
                nc.tensor.matmul(
                    out=hgp[:, i, :],
                    lhsT=sel_bf[:, i, :],
                    rhs=h2t[:, h * HALF : h * HALF + G_COLS],
                    start=True,
                    stop=True,
                )
            return hgp

        def multiply_gp(r, t0, nt):
            h, i = divmod(r, NI)
            gw = gpsimd_cols(r)
            if r not in zb_of:
                zb_of[r] = zbp.tile([P, NT, HALF * 4], BF16, name="zb", align_bytes=64)
            nc.gpsimd.tensor_tensor(
                out=zb_of[r][:, t0 : t0 + nt, 0 : gw * 4].rearrange("p t (w j) -> p t w j", j=4),
                in0=xg[:, t0 : t0 + nt, h * HALF : h * HALF + gw, :],
                in1=hgs[:, h, i, 0:gw].unsqueeze(1).unsqueeze(3).to_broadcast([P, nt, gw, 4]),
                op=MULT,
            )

        zt_of = {}

        def scale_rows(r):
            i = r % NI
            zt_of[r] = ztp.tile([P, 2 * NT, 16, 16], BF16, name="zt")
            for f in range(16):
                nc.scalar.activation(
                    out=zt_of[r][:, :, f, :],
                    in_=xt[:].rearrange("p s g e -> p s (g e)"),
                    func=COPY,
                    scale=ht[:, 16 * i + f : 16 * i + f + 1],
                )

        def turn_rows(r):
            zp = miscp.tile([P, 2 * NT, P], F32, name="zp", tag="misc")
            for s in range(2 * NT):
                nc.tensor.transpose(
                    out=zp[:, s, :],
                    in_=zt_of[r][:, s, :, :].rearrange("p f g -> p (f g)").bitcast(F32),
                    identity=ident_f[:],
                )
            nc.scalar.copy(
                out=zb_of[r][:]
                .rearrange("p t w -> p (t w)")
                .bitcast(F32)
                .rearrange("p (t w a) -> p t w a", t=NT, a=2)[:, :, HALF - S_COLS :, :],
                in_=zp[:].rearrange("p (t a) n -> p t n a", t=NT),
            )

        def multiply(r, t, w0, nw):
            h = r // NI
            nc.vector.tensor_tensor(
                out=zb_of[r][:, t, w0 * 4 : (w0 + nw) * 4].rearrange(
                    "p (w a e) -> p w a e", a=2, e=2
                ),
                in0=xg[:, t, h * HALF + w0 : h * HALF + w0 + nw, :].rearrange(
                    "p w (a e) -> p w a e", a=2
                ),
                in1=hps_of[r][:, w0 : w0 + nw]
                .bitcast(BF16)
                .rearrange("p (w e) -> p w e", e=2)
                .unsqueeze(2)
                .to_broadcast([P, nw, 2, 2]),
                op=MULT,
            )

        def quantise_z(r, c0, ncol):
            if r not in zq_of:
                zc = zcp.tile([P, NT * HALF], U32, name="zc", align_bytes=64)
                zs = zcp.tile([P, NT * HALF], U8, name="zs", align_bytes=64)
                zq_of[r] = (zc, zs)
            zc, zs = zq_of[r]
            nc.vector.quantize_mx(
                out=zc[:, c0 : c0 + ncol].bitcast(FP8X4),
                scales=zs[:, c0 : c0 + ncol],
                in_=zb_of[r][:].rearrange("p t w -> p (t w)")[:, 4 * c0 : 4 * (c0 + ncol)],
            )

        def contract(r, t, w0, nw, group):
            s = NT * (r % NI) + t
            zc, zs = zq_of[r]
            for ct in range(2):
                nc.tensor.matmul_mx(
                    out=group[ct][:],
                    lhsT=wc[:, s, ct * P : (ct + 1) * P].bitcast(FP8X4),
                    lhsT_scale=ws[:, s, ct * P : (ct + 1) * P],
                    rhs=zc[:, t * HALF + w0 : t * HALF + w0 + nw].bitcast(FP8X4),
                    rhs_scale=zs[:, t * HALF + w0 : t * HALF + w0 + nw],
                    start=(s == 0),
                    stop=(s == NI * NT - 1),
                )

        def pool_first_half():
            for ct in range(2):
                nc.scalar.activation(
                    out=y0[:, ct, :, :].rearrange("p b d -> p (b d)"),
                    in_=acc_h0[ct][:],
                    func=RELU,
                    bias=b3f[:, ct : ct + 1],
                    scale=1.0,
                )
            acc_q[3] = [
                accp.tile([P, QUART], F32, name="acc_q3_%d" % ct, tag="a%d" % ct) for ct in range(2)
            ]

        def fold(out, in_):
            n = in_.shape[-1] // 2
            nc.gpsimd.tensor_tensor(out=out, in0=in_[:, :, 0:n], in1=in_[:, :, n : 2 * n], op=ADD)

        def sum_first_half_begin(ct):
            fold(y1[:, ct, :, :], y0[:, ct, :, :])

        def sum_first_half_end():
            tail = zbp.tile([P, NT, HALF * 4], BF16, name="zb", align_bytes=64)
            words = tail[:].rearrange("p t w -> p (t w)").bitcast(F32)
            part, at = y1[:].rearrange("p ct b d -> p (ct b) d"), 0
            for n in (8, 4, 2):
                nxt = words[:, at : at + 2 * 16 * n].rearrange("p (s d) -> p s d", d=n)
                fold(nxt, part)
                part, at = nxt, at + 2 * 16 * n
            for ct in range(2):
                fold(
                    res[:, ct * NB : ct * NB + 16].unsqueeze(2), part[:, 16 * ct : 16 * ct + 16, :]
                )

        def pool_quarter(q):
            for ct in range(2):
                y = epi.tile([P, 8, ND], F32, name="y")
                nc.scalar.activation(
                    out=y[:].rearrange("p b d -> p (b d)"),
                    in_=acc_q[q][ct][:],
                    func=RELU,
                    bias=b3f[:, ct : ct + 1],
                    scale=1.0,
                )
                nc.vector.tensor_reduce(
                    out=res[:, ct * NB + 8 * q : ct * NB + 8 * q + 8],
                    in_=y[:],
                    axis=mybir.AxisListType.X,
                    op=ADD,
                )

        nc.scalar.dma_start(**load_h(0))
        load_x([nc.sync, nc.scalar] * 3 + [nc.sync] * 2, 0, 16, 0, 128)
        nc.gpsimd.memset(res[:], 0.0)
        nc.scalar.copy(out=junk[:, 0:1], in_=res[:, 0:1])
        load_x([nc.sync] * 8, 0, 16, 128, 128)
        nc.sync.dma_start(**load_h(1))
        for k in range(2):
            nc.sync.dma_start(
                out=xn[64 * k : 64 * k + 64, :].rearrange("p (b d) -> p b d", d=ND),
                in_=x0[NB - 4 - 4 * k : NB - 4 * k, :, :].rearrange("b g d -> g b d"),
            )
        for i in range(NI):
            nc.sync.dma_start(out=wraw[:, i, :], in_=wv[:, i, :])
        make_identity(nc, ident_bf[:])
        make_identity(nc, ident_f[:])
        nc.gpsimd.memset(bz[:], 0.0)
        nc.sync.dma_start(out=bz[0:2, :], in_=b3.rearrange("(ct c) -> ct c", ct=2))
        load_x([nc.sync] * 8, 16, 16 - S_COLS // ND, 0, 256)

        nc.vector.tensor_copy(
            out=sel_bf[:].rearrange("p i (ph r) -> p i ph r", r=8),
            in_=ident_bf[:]
            .rearrange("p (i ph) -> p i ph", i=NI)
            .unsqueeze(3)
            .to_broadcast([P, NI, 16, 8]),
        )
        nc.vector.tensor_copy(
            out=sel[:].rearrange("p i (ph r) -> p i ph r", r=8),
            in_=ident_f[:]
            .rearrange("p (i ph) -> p i ph", i=NI)
            .unsqueeze(3)
            .to_broadcast([P, NI, 16, 8]),
        )
        dup_h(nc.vector.tensor_copy, G_COLS, QUART - G_COLS)
        dup_h(nc.vector.tensor_copy, QUART, QUART)
        for r in range(H_AHEAD):
            spread_h(r)
        hgp0 = spread_h_gp(0)

        regroup_x(nc.scalar.copy, 0, 8, 8)
        nc.scalar.copy(out=hgs[:, 0, :, :], in_=hgp0[:])
        regroup_x(nc.scalar.copy, 1, 0, 8)
        regroup_x(nc.scalar.copy, 1, 8, 8)
        regroup_w(0)
        regroup_w(1)
        dup_h(nc.scalar.copy, HALF + G_COLS_S, HALF - S_COLS - G_COLS_S)
        hgp1 = spread_h_gp(1)
        nc.scalar.copy(out=hgs[:, 1, :, :], in_=hgp1[:])
        for i in range(2, 4):
            regroup_w(i)

        regroup_x(nc.vector.tensor_copy, 0, 0, 8)
        for t in range(NT):
            for r in range(H_AHEAD):
                multiply_gp(r, t, 1)
                if r == 0:
                    multiply(r, t, G_COLS, QUART - G_COLS)
                    multiply(r, t, QUART, QUART)
                else:
                    multiply(r, t, G_COLS, HALF - G_COLS)
                if t == NT - 1:
                    spread_h(r + H_AHEAD)
        for r in range(H_AHEAD, G_LEAD):
            multiply_gp(r, 0, NT)

        contracted = 0
        w_done = 0
        for r in range(N_PAIRS - 1):
            if r < N_PAIRS - 3:
                quantise_z(r, 0, NT * HALF)
            else:
                for t in range(NT):
                    quantise_z(r, t * HALF, HALF)
            if r in W_ROUNDS:
                quantise_w(w_done // 2)
                w_done += 2
            if r + G_LEAD < N_PAIRS:
                multiply_gp(r + G_LEAD, 0, NT)
            if r == 1:
                turned = miscp.tile([P, 3, P], BF16, name="turned", tag="misc")
                for k, src in enumerate((xn[:], h2t[:, NW - S_COLS :], bz[:])):
                    nc.tensor.transpose(out=turned[:, k, :], in_=src, identity=ident_bf[:])
                nc.scalar.copy(
                    out=xt[:], in_=turned[:, 0, 0:64].rearrange("p (g s e) -> p s g e", g=8, e=2)
                )
                nc.scalar.copy(out=ht[:], in_=turned[:, 1, :])
                nc.scalar.copy(out=b3f[:], in_=turned[:, 2, 0:2])
                for t in range(NT):
                    regroup_x(nc.scalar.copy, t, 16, 16 - S_COLS // ND)
                for i in range(4, NI):
                    regroup_w(i)
                scale_rows(S_PAIRS[0])
            if r + 2 in S_PAIRS[:-1]:
                scale_rows(r + 3)
            if r + 2 in S_PAIRS[1:-1]:
                turn_rows(r + 2)
            if r == POOL_ROUND:
                pool_first_half()
            if r in SUM_ROUNDS:
                sum_first_half_begin(SUM_ROUNDS.index(r))
            if r == SUM_ROUNDS[-1] + 1:
                sum_first_half_end()
            while contracted <= r and contracted % NI < w_done and (contracted < NI or r >= POOL_ROUND):
                for t in range(NT):
                    if contracted < NI:
                        contract(contracted, t, 0, HALF, acc_h0)
                    else:
                        for q in (2, 3):
                            contract(contracted, t, (q - 2) * QUART, QUART, acc_q[q])
                contracted += 1
            if r + 3 == S_PAIRS[-1]:
                turn_rows(r + 3)
            if r + H_AHEAD < N_PAIRS:
                v0, v1 = vector_cols(r + H_AHEAD)
                for t in range(NT):
                    multiply(r + H_AHEAD, t, v0, v1 - v0)
                if r + 2 * H_AHEAD < N_PAIRS:
                    spread_h(r + 2 * H_AHEAD)
            if r + 2 == S_PAIRS[0]:
                turn_rows(r + 2)

        r = N_PAIRS - 1
        for q in (2, 3):
            for t in range(NT):
                quantise_z(r, t * HALF + (q - 2) * QUART, QUART)
        for q in (2, 3):
            for t in range(NT):
                contract(r, t, (q - 2) * QUART, QUART, acc_q[q])
        for q in (2, 3):
            pool_quarter(q)

        tps = miscp.tile([P, P], F32, name="tps", tag="misc")
        nc.tensor.transpose(out=tps[:], in_=res[:], identity=ident_f[:])
        nc.scalar.copy(out=o_sb[:], in_=tps[:])
        for ct in range(2):
            nc.sync.dma_start(
                out=out[:, ct * P : (ct + 1) * P], in_=o_sb[ct * NB : (ct + 1) * NB, :]
            )
